import numpy as np
import ml_dtypes


def mxq(x, axis, fmt="e4m3"):
    dtype, down = {"e4m3": (ml_dtypes.float8_e4m3fn, 7), "e5m2": (ml_dtypes.float8_e5m2, 14)}[fmt]
    v = np.moveaxis(np.asarray(x, np.float32).astype(ml_dtypes.bfloat16).astype(np.float64), axis, -1)
    blocks = v.reshape(v.shape[:-1] + (-1, 32))
    amax = np.abs(blocks).max(-1, keepdims=True)
    byte = np.maximum(np.where(amax > 0, np.frexp(amax)[1] - 1 + 127, 0) - down, 1)
    scale = np.exp2(byte - 127.0)
    codes = (blocks / scale).astype(np.float32).astype(dtype).astype(np.float64)
    return np.moveaxis((codes * scale).reshape(v.shape), -1, axis)


WIDE = False


def mx_kscale(k):
    if not WIDE:
        return np.ones(k)
    levels = np.array([20, -20, 10, -10, 0])
    a = np.random.permutation(np.resize(levels, k // 512 * 4)).reshape(k // 512, 4)
    idx = np.arange(k)
    return np.exp2(a[idx // 512, idx % 128 // 32])


BF16 = ml_dtypes.bfloat16


def bf(x):
    return np.asarray(x, np.float32).astype(BF16)


def f64(x):
    return np.asarray(x).astype(np.float64)


B, NI, NK, NJ, C_Z, C_H = 1, 512, 512, 512, 128, 8
EPS = 1e-5
KEEP = 0.85
G_SCALE = 8.0


def layer_norm(x, w, b):
    mu = x.mean(-1, keepdims=True)
    var = ((x - mu) ** 2).mean(-1, keepdims=True)
    return (x - mu) / np.sqrt(var + EPS) * w + b


def tri_product(a_gated, b_gated, mask_ik, mask_kj):
    a = f64(mask_ik)[..., None] * f64(a_gated)
    b = f64(mask_kj)[..., None] * f64(b_gated)
    return (a.transpose(0, 3, 1, 2) @ b.transpose(0, 3, 1, 2)).transpose(0, 2, 3, 1)


def setup_inputs():
    s = mx_kscale(NI)[None, :, None, None]
    a0 = bf(np.random.standard_normal((B, NI, NK, C_H)) * 0.55)
    b_gated = bf(np.random.standard_normal((B, NK, NJ, C_H)) * 0.55)
    mask_ik = bf(np.random.random((B, NI, NK)) < KEEP)
    mask_kj = bf(np.random.random((B, NK, NJ)) < KEEP)
    ln_out_w = bf(1.0 + 0.1 * np.random.standard_normal(C_H))
    ln_out_b = bf(0.1 * np.random.standard_normal(C_H))
    g = bf(np.random.standard_normal((B, NI, NJ, C_H)) * np.exp2(np.random.randint(-12, 1, (B, NI, NJ, 1))) * G_SCALE / s)
    x = tri_product(a0, b_gated, mask_ik, mask_kj)
    mu = x.mean(-1)
    var = ((x - mu[..., None]) ** 2).mean(-1)
    rstd = 1.0 / np.sqrt(var + EPS)
    return {"a_gated": bf(f64(a0) * s), "b_gated": b_gated, "mask_ik": mask_ik, "mask_kj": mask_kj,
            "ln_out_w": ln_out_w, "ln_out_b": ln_out_b,
            "x": np.asarray(x, np.float32), "mu": np.asarray(mu, np.float32), "rstd": np.asarray(rstd, np.float32),
            "grad_out": g}


def reference(a_gated, b_gated, mask_ik, mask_kj, ln_out_w, ln_out_b, x, mu, rstd, grad_out):
    a = f64(mask_ik)[..., None] * f64(a_gated)
    r = f64(rstd)[..., None]
    xhat = (f64(x) - f64(mu)[..., None]) * r
    h = f64(grad_out) * f64(ln_out_w)
    dx = r * (h - h.mean(-1, keepdims=True) - xhat * (h * xhat).mean(-1, keepdims=True))
    at = a.transpose(0, 3, 2, 1)
    dxt = dx.transpose(0, 3, 1, 2)
    db = (mxq(at, 3, "e4m3") @ mxq(dxt, 2, "e5m2")).transpose(0, 2, 3, 1)
    return f64(mask_kj)[..., None] * db

@@ -1,0 +1,260 @@
+import concourse.mybir as mybir
+from concourse.masks import make_identity
+
+F32 = mybir.dt.float32
+BF16 = mybir.dt.bfloat16
+U32 = mybir.dt.uint32
+U8 = mybir.dt.uint8
+E4M3_X4 = mybir.dt.float8_e4m3fn_x4
+E5M2_X4 = mybir.dt.float8_e5m2_x4
+ALU = mybir.AluOpType
+SQUARE = mybir.ActivationFunctionType.Square
+
+P = 128
+PACK = 4
+SIDE = 512
+CH = 8
+HALF_CH = 4
+J_STEP = 64
+STEPS = SIDE // J_STEP
+COLS = J_STEP * PACK
+K_TILE = 128
+K_TILES = SIDE // K_TILE
+
+FLOPS = 2 * CH * SIDE * SIDE * SIDE
+BYTES = SIDE * SIDE * (CH * (2 + 2 + 4 + 4) + 2 + 2 + 4 + 4) + 2 * CH
+
+
+def tile_trianglemultiplicativeupdate_pa_v_kernel(
+    tc, a_gated, b_gated, mask_ik, mask_kj, ln_out_w, ln_out_b, x, mu, rstd, grad_out, out
+):
+    nc = tc.nc
+
+    a_rows = a_gated[0].rearrange("(p t) k d -> p t k d", t=PACK)
+    mask_ik_rows = mask_ik[0].rearrange("(p t) k -> p t k", t=PACK)
+    x_rows = x[0].rearrange("(p t) j d -> p t j d", t=PACK)
+    g_rows = grad_out[0].rearrange("(p t) j d -> p t j d", t=PACK)
+    mu_rows = mu[0].rearrange("(p t) j -> p t j", t=PACK)
+    rstd_rows = rstd[0].rearrange("(p t) j -> p t j", t=PACK)
+    mask_kj_rows = mask_kj[0].rearrange("(kt p) j -> p kt j", p=P)
+    out_rows = out[0].rearrange("(kt p) j d -> kt p (j d)", p=P)
+
+    def to_planes(planes, loaded):
+        for d in range(0, CH, HALF_CH):
+            nc.scalar.copy(
+                out=planes[:, d : d + HALF_CH, :].rearrange("p d (c t) -> p c t d", t=PACK),
+                in_=loaded[:, :, :, d : d + HALF_CH].rearrange("p t c d -> p c t d"),
+            )
+
+    def over_planes(per_pair):
+        return per_pair.unsqueeze(1).to_broadcast([P, CH, COLS])
+
+    with tc.manual_schedule(), tc.tile_pool(name="keep", bufs=1) as keep:
+        a_codes = keep.tile([P, K_TILES, CH, K_TILE], U32, align_bytes=64)
+        a_scales = keep.tile([P, K_TILES, CH, K_TILE], U8, align_bytes=64)
+        dx_codes = keep.tile([P, CH, SIDE], U32, align_bytes=64)
+        dx_scales = keep.tile([P, CH, SIDE], U8, align_bytes=64)
+        mask_kj_sb = keep.tile([P, K_TILES, SIDE], BF16)
+
+        with tc.tile_pool(name="once", bufs=1) as once, tc.tile_pool(name="loads", bufs=2) as loads, tc.tile_pool(
+            name="work", bufs=2
+        ) as work, tc.psum_pool(name="sums", bufs=2) as sums:
+            identity = once.tile([P, P], F32)
+            make_identity(nc, identity[:])
+            w_bf16 = once.tile([P, CH], BF16)
+            nc.sync.dma_start(out=w_bf16[:], in_=ln_out_w.partition_broadcast(P))
+            w = once.tile([P, CH], F32)
+            nc.vector.tensor_copy(out=w[:], in_=w_bf16[:])
+            mask_ik_sb = once.tile([P, PACK, SIDE], BF16)
+
+            loaded = {}
+            ready = {}
+            state = {}
+
+            def load(s):
+                cols = slice(s * J_STEP, (s + 1) * J_STEP)
+                rstd_ld = loads.tile([P, PACK, J_STEP], F32)
+                nc.sync.dma_start(out=rstd_ld[:], in_=rstd_rows[:, :, cols])
+                g_ld = loads.tile([P, PACK, J_STEP, CH], BF16)
+                nc.sync.dma_start(out=g_ld[:], in_=g_rows[:, :, cols, :])
+                mu_ld = loads.tile([P, PACK, J_STEP], F32)
+                nc.sync.dma_start(out=mu_ld[:], in_=mu_rows[:, :, cols])
+                x_ld = loads.tile([P, PACK, J_STEP, CH], F32)
+                nc.sync.dma_start(out=x_ld[:], in_=x_rows[:, :, cols, :])
+                loaded[s] = (rstd_ld, g_ld, mu_ld, x_ld)
+
+            def lay_out(s):
+                rstd_ld, g_ld, mu_ld, x_ld = loaded[s]
+                r = work.tile([P, COLS], F32)
+                nc.scalar.copy(out=r[:].rearrange("p (j t) -> p j t", t=PACK), in_=rstd_ld[:].rearrange("p t j -> p j t"))
+                g = work.tile([P, CH, COLS], BF16)
+                to_planes(g, g_ld)
+                m = work.tile([P, COLS], F32)
+                nc.scalar.copy(out=m[:].rearrange("p (j t) -> p j t", t=PACK), in_=mu_ld[:].rearrange("p t j -> p j t"))
+                xc = work.tile([P, CH, COLS], F32, bufs=3)
+                to_planes(xc, x_ld)
+                r_sq = work.tile([P, COLS], F32, bufs=3)
+                nc.scalar.activation(out=r_sq[:], in_=r[:], func=SQUARE)
+                ready[s] = (r, g, m, xc, r_sq)
+
+            def sum_over_channels(planes):
+                turned = sums.tile([P, COLS], F32)
+                for b in range(0, COLS, P):
+                    for d in range(CH):
+                        nc.tensor.matmul(
+                            out=turned[:, b : b + P],
+                            lhsT=planes[:, d, b : b + P],
+                            rhs=identity[:],
+                            is_transpose=True,
+                            start=(d == 0),
+                            stop=(d == CH - 1),
+                        )
+                turned_sb = work.tile([P, COLS], F32)
+                nc.scalar.copy(out=turned_sb[:], in_=turned[:])
+                total = sums.tile([P, COLS], F32, bufs=4)
+                for b in range(0, COLS, P):
+                    nc.tensor.transpose(out=total[:, b : b + P], in_=turned_sb[:, b : b + P], identity=identity[:])
+                return total
+
+            def scale_grad(s):
+                r, g, m, xc, r_sq = ready[s]
+                hr = work.tile([P, CH, COLS], F32, bufs=3)
+                for d in range(CH):
+                    nc.vector.scalar_tensor_tensor(
+                        out=hr[:, d, :], in0=g[:, d, :], scalar=w[:, d : d + 1], in1=r[:], op0=ALU.mult, op1=ALU.mult
+                    )
+                state[s] = {"hr": hr, "sum_hr": sum_over_channels(hr)}
+
+            def centre_x(s):
+                r, g, m, xc, r_sq = ready[s]
+                nc.vector.tensor_tensor(out=xc[:], in0=xc[:], in1=over_planes(m[:]), op=ALU.subtract)
+
+            def correlate(s):
+                xc = ready[s][3]
+                prod = work.tile([P, CH, COLS], F32)
+                nc.vector.tensor_tensor(out=prod[:], in0=state[s]["hr"][:], in1=xc[:], op=ALU.mult)
+                state[s]["sum_prod"] = sum_over_channels(prod)
+
+            def slope(s):
+                kappa = work.tile([P, COLS], F32)
+                nc.vector.scalar_tensor_tensor(
+                    out=kappa[:], in0=state[s]["sum_prod"][:], scalar=1.0 / CH, in1=ready[s][4][:], op0=ALU.mult, op1=ALU.mult
+                )
+                state[s]["kappa"] = kappa
+
+            def scale_xc(s):
+                xc = ready[s][3]
+                nc.vector.tensor_tensor(out=xc[:], in0=xc[:], in1=over_planes(state[s]["kappa"][:]), op=ALU.mult)
+
+            def add_mean(s):
+                xc = ready[s][3]
+                nc.vector.scalar_tensor_tensor(
+                    out=xc[:], in0=over_planes(state[s]["sum_hr"][:]), scalar=1.0 / CH, in1=xc[:], op0=ALU.mult, op1=ALU.add
+                )
+
+            def finish_dx(s):
+                dx = work.tile([P, CH, COLS], BF16, align_bytes=64)
+                nc.vector.tensor_tensor(out=dx[:], in0=state[s]["hr"][:], in1=ready[s][3][:], op=ALU.subtract)
+                state[s]["dx"] = dx
+
+            def quantise_dx(s):
+                cols = slice(s * J_STEP, (s + 1) * J_STEP)
+                for d in range(CH):
+                    nc.vector.quantize_mx(
+                        out=dx_codes[:, d, cols].bitcast(E5M2_X4), scales=dx_scales[:, d, cols], in_=state[s]["dx"][:, d, :]
+                    )
+
+            a_tiles = {}
+
+            def load_a(kt):
+                a_ld = loads.tile([P, PACK, K_TILE, CH], BF16)
+                nc.sync.dma_start(out=a_ld[:], in_=a_rows[:, :, kt * K_TILE : (kt + 1) * K_TILE, :])
+                a_tiles[kt] = a_ld
+
+            def lay_out_a(kt):
+                a_planes = work.tile([P, CH, K_TILE * PACK], BF16, align_bytes=64)
+                to_planes(a_planes, a_tiles[kt])
+                keep_ik = work.tile([P, K_TILE * PACK], BF16)
+                nc.scalar.copy(
+                    out=keep_ik[:].rearrange("p (k t) -> p k t", t=PACK),
+                    in_=mask_ik_sb[:, :, kt * K_TILE : (kt + 1) * K_TILE].rearrange("p t k -> p k t"),
+                )
+                a_tiles[kt] = (a_planes, keep_ik)
+
+            def mask_a(kt):
+                a_planes, keep_ik = a_tiles[kt]
+                nc.vector.tensor_tensor(
+                    out=a_planes[:],
+                    in0=a_planes[:],
+                    in1=keep_ik[:].unsqueeze(1).to_broadcast([P, CH, K_TILE * PACK]),
+                    op=ALU.mult,
+                )
+
+            def quantise_a(kt):
+                nc.vector.quantize_mx(
+                    out=a_codes[:, kt, :, :].rearrange("p d k -> p (d k)").bitcast(E4M3_X4),
+                    scales=a_scales[:, kt, :, :].rearrange("p d k -> p (d k)"),
+                    in_=a_tiles[kt][0][:].rearrange("p d c -> p (d c)"),
+                )
+
+            load(0)
+            load(1)
+            nc.sync.dma_start(out=mask_ik_sb[:], in_=mask_ik_rows)
+            load_a(0)
+            lay_out(0)
+            for turn in range(STEPS + 2):
+                first, second, third = turn, turn - 1, turn - 2
+                kt = turn // 2
+                if turn + 2 < STEPS:
+                    load(turn + 2)
+                if turn % 2 == 0 and kt + 1 < K_TILES:
+                    load_a(kt + 1)
+                if turn == STEPS // 2:
+                    nc.sync.dma_start(out=mask_kj_sb[:], in_=mask_kj_rows)
+                if first < STEPS:
+                    scale_grad(first)
+                if first + 1 < STEPS:
+                    lay_out(first + 1)
+                if 0 <= second < STEPS:
+                    slope(second)
+                if first < STEPS:
+                    centre_x(first)
+                if 0 <= second < STEPS:
+                    scale_xc(second)
+                if first < STEPS:
+                    correlate(first)
+                if turn % 2 == 0 and kt < K_TILES:
+                    lay_out_a(kt)
+                if 0 <= second < STEPS:
+                    add_mean(second)
+                if 0 <= third:
+                    quantise_dx(third)
+                if turn % 2 == 1 and kt < K_TILES:
+                    mask_a(kt)
+                if 0 <= second < STEPS:
+                    finish_dx(second)
+                if turn % 2 == 1 and kt < K_TILES:
+                    quantise_a(kt)
+
+        with tc.tile_pool(name="tail", bufs=2) as tail, tc.psum_pool(name="products", bufs=8) as products:
+            for kt in range(K_TILES):
+                masked = tail.tile([P, CH, SIDE], F32)
+                woven = tail.tile([P, SIDE, CH], F32)
+                for d in range(CH):
+                    product = products.tile([P, SIDE], F32)
+                    nc.tensor.matmul_mx(
+                        out=product[:],
+                        lhsT=a_codes[:, kt, d, :].bitcast(E4M3_X4),
+                        lhsT_scale=a_scales[:, kt, d, :],
+                        rhs=dx_codes[:, d, :].bitcast(E5M2_X4),
+                        rhs_scale=dx_scales[:, d, :],
+                        start=True,
+                        stop=True,
+                    )
+                    nc.vector.tensor_tensor(out=masked[:, d, :], in0=product[:], in1=mask_kj_sb[:, kt, :], op=ALU.mult)
+                    if d % HALF_CH == HALF_CH - 1:
+                        lo = d + 1 - HALF_CH
+                        nc.scalar.copy(
+                            out=woven[:, :, lo : lo + HALF_CH], in_=masked[:, lo : lo + HALF_CH, :].rearrange("p d j -> p j d")
+                        )
+                nc.sync.dma_start(out=out_rows[kt], in_=woven[:].rearrange("p j d -> p (j d)"))

@@ -46,8 +46,8 @@ def tile_trianglemultiplicativeupdate_pa_v_kernel(
                 in_=loaded[:, :, :, d : d + HALF_CH].rearrange("p t c d -> p c t d"),
             )
 
-    def over_planes(per_pair):
-        return per_pair.unsqueeze(1).to_broadcast([P, CH, COLS])
+    def over_planes(per_pair, count):
+        return per_pair.unsqueeze(1).to_broadcast([P, count, COLS])
 
     with tc.manual_schedule(), tc.tile_pool(name="keep", bufs=1) as keep:
         a_codes = keep.tile([P, K_TILES, CH, K_TILE], U32, align_bytes=64)
@@ -75,86 +75,108 @@ def tile_trianglemultiplicativeupdate_pa_v_kernel(
                 cols = slice(s * J_STEP, (s + 1) * J_STEP)
                 rstd_ld = loads.tile([P, PACK, J_STEP], F32)
                 nc.sync.dma_start(out=rstd_ld[:], in_=rstd_rows[:, :, cols])
-                g_ld = loads.tile([P, PACK, J_STEP, CH], BF16)
-                nc.sync.dma_start(out=g_ld[:], in_=g_rows[:, :, cols, :])
                 mu_ld = loads.tile([P, PACK, J_STEP], F32)
                 nc.sync.dma_start(out=mu_ld[:], in_=mu_rows[:, :, cols])
                 x_ld = loads.tile([P, PACK, J_STEP, CH], F32)
                 nc.sync.dma_start(out=x_ld[:], in_=x_rows[:, :, cols, :])
+                g_ld = loads.tile([P, PACK, J_STEP, CH], BF16)
+                nc.sync.dma_start(out=g_ld[:], in_=g_rows[:, :, cols, :])
                 loaded[s] = (rstd_ld, g_ld, mu_ld, x_ld)
 
-            def lay_out(s):
-                rstd_ld, g_ld, mu_ld, x_ld = loaded[s]
-                r = work.tile([P, COLS], F32)
-                nc.scalar.copy(out=r[:].rearrange("p (j t) -> p j t", t=PACK), in_=rstd_ld[:].rearrange("p t j -> p j t"))
-                g = work.tile([P, CH, COLS], BF16)
-                to_planes(g, g_ld)
-                m = work.tile([P, COLS], F32)
-                nc.scalar.copy(out=m[:].rearrange("p (j t) -> p j t", t=PACK), in_=mu_ld[:].rearrange("p t j -> p j t"))
-                xc = work.tile([P, CH, COLS], F32, bufs=3)
-                to_planes(xc, x_ld)
-                r_sq = work.tile([P, COLS], F32, bufs=3)
-                nc.scalar.activation(out=r_sq[:], in_=r[:], func=SQUARE)
-                ready[s] = (r, g, m, xc, r_sq)
-
-            def sum_over_channels(planes):
-                turned = sums.tile([P, COLS], F32)
+            def turn_and_add(planes, count):
+                turned = sums.tile([P, COLS], F32, bufs=3)
                 for b in range(0, COLS, P):
-                    for d in range(CH):
+                    for d in range(count):
                         nc.tensor.matmul(
                             out=turned[:, b : b + P],
                             lhsT=planes[:, d, b : b + P],
                             rhs=identity[:],
                             is_transpose=True,
                             start=(d == 0),
-                            stop=(d == CH - 1),
+                            stop=(d == count - 1),
                         )
-                turned_sb = work.tile([P, COLS], F32)
-                nc.scalar.copy(out=turned_sb[:], in_=turned[:])
-                total = sums.tile([P, COLS], F32, bufs=4)
+                return turned
+
+            def turn_back(turned_sb):
+                straight = sums.tile([P, COLS], F32, bufs=4)
                 for b in range(0, COLS, P):
-                    nc.tensor.transpose(out=total[:, b : b + P], in_=turned_sb[:, b : b + P], identity=identity[:])
-                return total
+                    nc.tensor.transpose(out=straight[:, b : b + P], in_=turned_sb[:, b : b + P], identity=identity[:])
+                return straight
+
+            def lay_out(s):
+                rstd_ld, g_ld, mu_ld, x_ld = loaded[s]
+                r = work.tile([P, 1, COLS], F32)
+                nc.scalar.copy(
+                    out=r[:, 0, :].rearrange("p (j t) -> p j t", t=PACK), in_=rstd_ld[:].rearrange("p t j -> p j t")
+                )
+                m = work.tile([P, COLS], F32)
+                nc.scalar.copy(out=m[:].rearrange("p (j t) -> p j t", t=PACK), in_=mu_ld[:].rearrange("p t j -> p j t"))
+                xc = work.tile([P, CH, COLS], F32, bufs=3)
+                to_planes(xc, x_ld)
+                g = work.tile([P, CH, COLS], BF16)
+                to_planes(g, g_ld)
+                r_sq_turned = work.tile([P, COLS], F32, bufs=3)
+                nc.scalar.activation(out=r_sq_turned[:], in_=turn_and_add(r, 1)[:], func=SQUARE)
+                ready[s] = (r, g, m, xc, r_sq_turned)
+
+            def centre_x(s):
+                r, g, m, xc, r_sq_turned = ready[s]
+                nc.vector.tensor_tensor(out=xc[:], in0=xc[:], in1=over_planes(m[:], CH), op=ALU.subtract)
 
             def scale_grad(s):
-                r, g, m, xc, r_sq = ready[s]
+                r, g, m, xc, r_sq_turned = ready[s]
                 hr = work.tile([P, CH, COLS], F32, bufs=3)
                 for d in range(CH):
                     nc.vector.scalar_tensor_tensor(
-                        out=hr[:, d, :], in0=g[:, d, :], scalar=w[:, d : d + 1], in1=r[:], op0=ALU.mult, op1=ALU.mult
+                        out=hr[:, d, :], in0=g[:, d, :], scalar=w[:, d : d + 1], in1=r[:, 0, :], op0=ALU.mult, op1=ALU.mult
                     )
-                state[s] = {"hr": hr, "sum_hr": sum_over_channels(hr)}
-
-            def centre_x(s):
-                r, g, m, xc, r_sq = ready[s]
-                nc.vector.tensor_tensor(out=xc[:], in0=xc[:], in1=over_planes(m[:]), op=ALU.subtract)
+                sum_turned = work.tile([P, COLS], F32)
+                nc.scalar.copy(out=sum_turned[:], in_=turn_and_add(hr, CH)[:])
+                state[s] = {"hr": hr, "sum_hr": turn_back(sum_turned)}
 
             def correlate(s):
-                xc = ready[s][3]
                 prod = work.tile([P, CH, COLS], F32)
-                nc.vector.tensor_tensor(out=prod[:], in0=state[s]["hr"][:], in1=xc[:], op=ALU.mult)
-                state[s]["sum_prod"] = sum_over_channels(prod)
+                nc.gpsimd.tensor_tensor(out=prod[:], in0=state[s]["hr"][:], in1=ready[s][3][:], op=ALU.mult)
+                state[s]["sum_prod_turned"] = turn_and_add(prod, CH)
 
             def slope(s):
-                kappa = work.tile([P, COLS], F32)
+                kappa_turned = work.tile([P, COLS], F32)
                 nc.vector.scalar_tensor_tensor(
-                    out=kappa[:], in0=state[s]["sum_prod"][:], scalar=1.0 / CH, in1=ready[s][4][:], op0=ALU.mult, op1=ALU.mult
+                    out=kappa_turned[:],
+                    in0=state[s]["sum_prod_turned"][:],
+                    scalar=1.0 / CH,
+                    in1=ready[s][4][:],
+                    op0=ALU.mult,
+                    op1=ALU.mult,
                 )
-                state[s]["kappa"] = kappa
+                state[s]["kappa"] = turn_back(kappa_turned)
 
             def scale_xc(s):
-                xc = ready[s][3]
-                nc.vector.tensor_tensor(out=xc[:], in0=xc[:], in1=over_planes(state[s]["kappa"][:]), op=ALU.mult)
+                for lo in range(0, CH, HALF_CH):
+                    part = ready[s][3][:, lo : lo + HALF_CH, :]
+                    nc.vector.tensor_tensor(out=part, in0=part, in1=over_planes(state[s]["kappa"][:], HALF_CH), op=ALU.mult)
 
             def add_mean(s):
-                xc = ready[s][3]
-                nc.vector.scalar_tensor_tensor(
-                    out=xc[:], in0=over_planes(state[s]["sum_hr"][:]), scalar=1.0 / CH, in1=xc[:], op0=ALU.mult, op1=ALU.add
-                )
+                for lo in range(0, CH, HALF_CH):
+                    part = ready[s][3][:, lo : lo + HALF_CH, :]
+                    nc.vector.scalar_tensor_tensor(
+                        out=part,
+                        in0=over_planes(state[s]["sum_hr"][:], HALF_CH),
+                        scalar=1.0 / CH,
+                        in1=part,
+                        op0=ALU.mult,
+                        op1=ALU.add,
+                    )
 
             def finish_dx(s):
                 dx = work.tile([P, CH, COLS], BF16, align_bytes=64)
-                nc.vector.tensor_tensor(out=dx[:], in0=state[s]["hr"][:], in1=ready[s][3][:], op=ALU.subtract)
+                for lo in range(0, CH, HALF_CH):
+                    nc.vector.tensor_tensor(
+                        out=dx[:, lo : lo + HALF_CH, :],
+                        in0=state[s]["hr"][:, lo : lo + HALF_CH, :],
+                        in1=ready[s][3][:, lo : lo + HALF_CH, :],
+                        op=ALU.subtract,
+                    )
                 state[s]["dx"] = dx
 
             def quantise_dx(s):
@@ -211,28 +233,25 @@ def tile_trianglemultiplicativeupdate_pa_v_kernel(
                     load_a(kt + 1)
                 if turn == STEPS // 2:
                     nc.sync.dma_start(out=mask_kj_sb[:], in_=mask_kj_rows)
-                if first < STEPS:
-                    scale_grad(first)
                 if first + 1 < STEPS:
                     lay_out(first + 1)
-                if 0 <= second < STEPS:
-                    slope(second)
                 if first < STEPS:
                     centre_x(first)
                 if 0 <= second < STEPS:
-                    scale_xc(second)
+                    slope(second)
                 if first < STEPS:
+                    scale_grad(first)
                     correlate(first)
                 if turn % 2 == 0 and kt < K_TILES:
                     lay_out_a(kt)
                 if 0 <= second < STEPS:
+                    scale_xc(second)
                     add_mean(second)
-                if 0 <= third:
-                    quantise_dx(third)
+                    finish_dx(second)
                 if turn % 2 == 1 and kt < K_TILES:
                     mask_a(kt)
-                if 0 <= second < STEPS:
-                    finish_dx(second)
+                if 0 <= third:
+                    quantise_dx(third)
                 if turn % 2 == 1 and kt < K_TILES:
                     quantise_a(kt)
 

@@ -13,6 +13,7 @@ SQUARE = mybir.ActivationFunctionType.Square
 P = 128
 PACK = 4
 SIDE = 512
+HALF_SIDE = SIDE // 2
 CH = 8
 HALF_CH = 4
 J_STEP = 64
@@ -68,7 +69,7 @@ def tile_trianglemultiplicativeupdate_pa_v_kernel(
             mask_ik_sb = once.tile([P, PACK, SIDE], BF16)
 
             loaded = {}
-            ready = {}
+            planes_g = {}
             state = {}
 
             def load(s):
@@ -77,10 +78,10 @@ def tile_trianglemultiplicativeupdate_pa_v_kernel(
                 nc.sync.dma_start(out=rstd_ld[:], in_=rstd_rows[:, :, cols])
                 mu_ld = loads.tile([P, PACK, J_STEP], F32)
                 nc.sync.dma_start(out=mu_ld[:], in_=mu_rows[:, :, cols])
-                x_ld = loads.tile([P, PACK, J_STEP, CH], F32)
-                nc.sync.dma_start(out=x_ld[:], in_=x_rows[:, :, cols, :])
                 g_ld = loads.tile([P, PACK, J_STEP, CH], BF16)
                 nc.sync.dma_start(out=g_ld[:], in_=g_rows[:, :, cols, :])
+                x_ld = loads.tile([P, PACK, J_STEP, CH], F32)
+                nc.sync.dma_start(out=x_ld[:], in_=x_rows[:, :, cols, :])
                 loaded[s] = (rstd_ld, g_ld, mu_ld, x_ld)
 
             def turn_and_add(planes, count):
@@ -98,12 +99,12 @@ def tile_trianglemultiplicativeupdate_pa_v_kernel(
                 return turned
 
             def turn_back(turned_sb):
-                straight = sums.tile([P, COLS], F32, bufs=4)
+                straight = sums.tile([P, COLS], F32, bufs=3)
                 for b in range(0, COLS, P):
                     nc.tensor.transpose(out=straight[:, b : b + P], in_=turned_sb[:, b : b + P], identity=identity[:])
                 return straight
 
-            def lay_out(s):
+            def lay_out_pairs(s):
                 rstd_ld, g_ld, mu_ld, x_ld = loaded[s]
                 r = work.tile([P, 1, COLS], F32)
                 nc.scalar.copy(
@@ -111,32 +112,54 @@ def tile_trianglemultiplicativeupdate_pa_v_kernel(
                 )
                 m = work.tile([P, COLS], F32)
                 nc.scalar.copy(out=m[:].rearrange("p (j t) -> p j t", t=PACK), in_=mu_ld[:].rearrange("p t j -> p j t"))
-                xc = work.tile([P, CH, COLS], F32, bufs=3)
-                to_planes(xc, x_ld)
-                g = work.tile([P, CH, COLS], BF16)
-                to_planes(g, g_ld)
-                r_sq_turned = work.tile([P, COLS], F32, bufs=3)
-                nc.scalar.activation(out=r_sq_turned[:], in_=turn_and_add(r, 1)[:], func=SQUARE)
-                ready[s] = (r, g, m, xc, r_sq_turned)
+                mu_rstd = sums.tile([P, 2, COLS], F32)
+                nc.tensor.matmul(out=mu_rstd[:, 1, :], lhsT=identity[:], rhs=r[:, 0, :], start=True, stop=True)
+                nc.tensor.matmul(out=mu_rstd[:, 0, :], lhsT=identity[:], rhs=m[:], start=True, stop=True)
+                state[s] = {"mu_rstd": mu_rstd, "r_turned": turn_and_add(r, 1)}
 
-            def centre_x(s):
-                r, g, m, xc, r_sq_turned = ready[s]
-                nc.vector.tensor_tensor(out=xc[:], in0=xc[:], in1=over_planes(m[:], CH), op=ALU.subtract)
+            def square_rstd(s):
+                r_sq_turned = work.tile([P, COLS], F32, bufs=3)
+                nc.scalar.activation(out=r_sq_turned[:], in_=state[s]["r_turned"][:], func=SQUARE)
+                state[s]["r_sq_turned"] = r_sq_turned
+
+            def lay_out_g(s):
+                g = work.tile([P, CH, COLS], BF16)
+                to_planes(g, loaded[s][1])
+                planes_g[s] = g
+
+            def lay_out_x(s):
+                xc = work.tile([P, CH, COLS], F32, bufs=3)
+                to_planes(xc, loaded[s][3])
+                state[s]["xc"] = xc
 
             def scale_grad(s):
-                r, g, m, xc, r_sq_turned = ready[s]
                 hr = work.tile([P, CH, COLS], F32, bufs=3)
                 for d in range(CH):
                     nc.vector.scalar_tensor_tensor(
-                        out=hr[:, d, :], in0=g[:, d, :], scalar=w[:, d : d + 1], in1=r[:, 0, :], op0=ALU.mult, op1=ALU.mult
+                        out=hr[:, d, :],
+                        in0=planes_g[s][:, d, :],
+                        scalar=w[:, d : d + 1],
+                        in1=state[s]["mu_rstd"][:, 1, :],
+                        op0=ALU.mult,
+                        op1=ALU.mult,
                     )
+                state[s]["hr"] = hr
+
+            def add_up_hr(s):
                 sum_turned = work.tile([P, COLS], F32)
-                nc.scalar.copy(out=sum_turned[:], in_=turn_and_add(hr, CH)[:])
-                state[s] = {"hr": hr, "sum_hr": turn_back(sum_turned)}
+                nc.scalar.copy(out=sum_turned[:], in_=turn_and_add(state[s]["hr"], CH)[:])
+                state[s]["sum_hr_turned"] = sum_turned
+
+            def turn_back_hr(s):
+                state[s]["sum_hr"] = turn_back(state[s]["sum_hr_turned"])
+
+            def centre_x(s):
+                xc = state[s]["xc"]
+                nc.vector.tensor_tensor(out=xc[:], in0=xc[:], in1=over_planes(state[s]["mu_rstd"][:, 0, :], CH), op=ALU.subtract)
 
             def correlate(s):
                 prod = work.tile([P, CH, COLS], F32)
-                nc.gpsimd.tensor_tensor(out=prod[:], in0=state[s]["hr"][:], in1=ready[s][3][:], op=ALU.mult)
+                nc.gpsimd.tensor_tensor(out=prod[:], in0=state[s]["hr"][:], in1=state[s]["xc"][:], op=ALU.mult)
                 state[s]["sum_prod_turned"] = turn_and_add(prod, CH)
 
             def slope(s):
@@ -145,7 +168,7 @@ def tile_trianglemultiplicativeupdate_pa_v_kernel(
                     out=kappa_turned[:],
                     in0=state[s]["sum_prod_turned"][:],
                     scalar=1.0 / CH,
-                    in1=ready[s][4][:],
+                    in1=state[s]["r_sq_turned"][:],
                     op0=ALU.mult,
                     op1=ALU.mult,
                 )
@@ -153,12 +176,12 @@ def tile_trianglemultiplicativeupdate_pa_v_kernel(
 
             def scale_xc(s):
                 for lo in range(0, CH, HALF_CH):
-                    part = ready[s][3][:, lo : lo + HALF_CH, :]
+                    part = state[s]["xc"][:, lo : lo + HALF_CH, :]
                     nc.vector.tensor_tensor(out=part, in0=part, in1=over_planes(state[s]["kappa"][:], HALF_CH), op=ALU.mult)
 
             def add_mean(s):
                 for lo in range(0, CH, HALF_CH):
-                    part = ready[s][3][:, lo : lo + HALF_CH, :]
+                    part = state[s]["xc"][:, lo : lo + HALF_CH, :]
                     nc.vector.scalar_tensor_tensor(
                         out=part,
                         in0=over_planes(state[s]["sum_hr"][:], HALF_CH),
@@ -168,15 +191,9 @@ def tile_trianglemultiplicativeupdate_pa_v_kernel(
                         op1=ALU.add,
                     )
 
-            def finish_dx(s):
-                dx = work.tile([P, CH, COLS], BF16, align_bytes=64)
-                for lo in range(0, CH, HALF_CH):
-                    nc.vector.tensor_tensor(
-                        out=dx[:, lo : lo + HALF_CH, :],
-                        in0=state[s]["hr"][:, lo : lo + HALF_CH, :],
-                        in1=ready[s][3][:, lo : lo + HALF_CH, :],
-                        op=ALU.subtract,
-                    )
+            def finish_dx(s, engine):
+                dx = work.tile([P, CH, COLS], BF16, align_bytes=64, bufs=1)
+                engine.tensor_tensor(out=dx[:], in0=state[s]["hr"][:], in1=state[s]["xc"][:], op=ALU.subtract)
                 state[s]["dx"] = dx
 
             def quantise_dx(s):
@@ -223,7 +240,10 @@ def tile_trianglemultiplicativeupdate_pa_v_kernel(
             load(1)
             nc.sync.dma_start(out=mask_ik_sb[:], in_=mask_ik_rows)
             load_a(0)
-            lay_out(0)
+            lay_out_pairs(0)
+            lay_out_g(0)
+            lay_out_x(0)
+            square_rstd(0)
             for turn in range(STEPS + 2):
                 first, second, third = turn, turn - 1, turn - 2
                 kt = turn // 2
@@ -233,32 +253,41 @@ def tile_trianglemultiplicativeupdate_pa_v_kernel(
                     load_a(kt + 1)
                 if turn == STEPS // 2:
                     nc.sync.dma_start(out=mask_kj_sb[:], in_=mask_kj_rows)
+                if 0 <= third:
+                    finish_dx(third, nc.gpsimd if third < STEPS - 1 else nc.vector)
                 if first + 1 < STEPS:
-                    lay_out(first + 1)
+                    lay_out_g(first + 1)
                 if first < STEPS:
-                    centre_x(first)
+                    scale_grad(first)
                 if 0 <= second < STEPS:
                     slope(second)
                 if first < STEPS:
-                    scale_grad(first)
+                    add_up_hr(first)
+                if first + 1 < STEPS:
+                    lay_out_pairs(first + 1)
+                if first < STEPS:
+                    turn_back_hr(first)
+                    centre_x(first)
                     correlate(first)
+                if first + 1 < STEPS:
+                    square_rstd(first + 1)
+                    lay_out_x(first + 1)
                 if turn % 2 == 0 and kt < K_TILES:
                     lay_out_a(kt)
                 if 0 <= second < STEPS:
                     scale_xc(second)
                     add_mean(second)
-                    finish_dx(second)
                 if turn % 2 == 1 and kt < K_TILES:
                     mask_a(kt)
+                    quantise_a(kt)
                 if 0 <= third:
                     quantise_dx(third)
-                if turn % 2 == 1 and kt < K_TILES:
-                    quantise_a(kt)
 
         with tc.tile_pool(name="tail", bufs=2) as tail, tc.psum_pool(name="products", bufs=8) as products:
             for kt in range(K_TILES):
                 masked = tail.tile([P, CH, SIDE], F32)
-                woven = tail.tile([P, SIDE, CH], F32)
+                woven_left = tail.tile([P, HALF_SIDE, CH], F32)
+                woven_right = tail.tile([P, HALF_SIDE, CH], F32)
                 for d in range(CH):
                     product = products.tile([P, SIDE], F32)
                     nc.tensor.matmul_mx(
@@ -274,6 +303,16 @@ def tile_trianglemultiplicativeupdate_pa_v_kernel(
                     if d % HALF_CH == HALF_CH - 1:
                         lo = d + 1 - HALF_CH
                         nc.scalar.copy(
-                            out=woven[:, :, lo : lo + HALF_CH], in_=masked[:, lo : lo + HALF_CH, :].rearrange("p d j -> p j d")
+                            out=woven_left[:, :, lo : lo + HALF_CH],
+                            in_=masked[:, lo : lo + HALF_CH, :HALF_SIDE].rearrange("p d j -> p j d"),
                         )
-                nc.sync.dma_start(out=out_rows[kt], in_=woven[:].rearrange("p j d -> p (j d)"))
+                        nc.gpsimd.tensor_scalar(
+                            out=woven_right[:, :, lo : lo + HALF_CH],
+                            in0=masked[:, lo : lo + HALF_CH, HALF_SIDE:].rearrange("p d j -> p j d"),
+                            scalar1=1.0,
+                            scalar2=0.0,
+                            op0=ALU.mult,
+                            op1=ALU.add,
+                        )
+                nc.sync.dma_start(out=out_rows[kt][:, : HALF_SIDE * CH], in_=woven_left[:].rearrange("p j d -> p (j d)"))
+                nc.sync.dma_start(out=out_rows[kt][:, HALF_SIDE * CH :], in_=woven_right[:].rearrange("p j d -> p (j d)"))

@@ -9,6 +9,7 @@ E4M3_X4 = mybir.dt.float8_e4m3fn_x4
 E5M2_X4 = mybir.dt.float8_e5m2_x4
 ALU = mybir.AluOpType
 SQUARE = mybir.ActivationFunctionType.Square
+COPY = mybir.ActivationFunctionType.Copy
 
 P = 128
 PACK = 4
@@ -70,6 +71,7 @@ def tile_trianglemultiplicativeupdate_pa_v_kernel(
 
             loaded = {}
             planes_g = {}
+            planes_x = {}
             state = {}
 
             def load(s):
@@ -98,12 +100,6 @@ def tile_trianglemultiplicativeupdate_pa_v_kernel(
                         )
                 return turned
 
-            def turn_back(turned_sb):
-                straight = sums.tile([P, COLS], F32, bufs=3)
-                for b in range(0, COLS, P):
-                    nc.tensor.transpose(out=straight[:, b : b + P], in_=turned_sb[:, b : b + P], identity=identity[:])
-                return straight
-
             def lay_out_pairs(s):
                 rstd_ld, g_ld, mu_ld, x_ld = loaded[s]
                 r = work.tile([P, 1, COLS], F32)
@@ -114,8 +110,9 @@ def tile_trianglemultiplicativeupdate_pa_v_kernel(
                 nc.scalar.copy(out=m[:].rearrange("p (j t) -> p j t", t=PACK), in_=mu_ld[:].rearrange("p t j -> p j t"))
                 mu_rstd = sums.tile([P, 2, COLS], F32)
                 nc.tensor.matmul(out=mu_rstd[:, 1, :], lhsT=identity[:], rhs=r[:, 0, :], start=True, stop=True)
-                nc.tensor.matmul(out=mu_rstd[:, 0, :], lhsT=identity[:], rhs=m[:], start=True, stop=True)
-                state[s] = {"mu_rstd": mu_rstd, "r_turned": turn_and_add(r, 1)}
+                for b in range(0, COLS, P):
+                    nc.tensor.transpose(out=mu_rstd[:, 0, b : b + P], in_=m[:, b : b + P], identity=identity[:])
+                state[s] = {"mu_rstd": mu_rstd, "m": m, "r_turned": turn_and_add(r, 1)}
 
             def square_rstd(s):
                 r_sq_turned = work.tile([P, COLS], F32, bufs=3)
@@ -128,13 +125,16 @@ def tile_trianglemultiplicativeupdate_pa_v_kernel(
                 planes_g[s] = g
 
             def lay_out_x(s):
-                xc = work.tile([P, CH, COLS], F32, bufs=3)
+                xc = work.tile([P, CH, COLS], F32, bufs=4)
                 to_planes(xc, loaded[s][3])
-                state[s]["xc"] = xc
+                planes_x[s] = xc
 
-            def scale_grad(s):
-                hr = work.tile([P, CH, COLS], F32, bufs=3)
-                for d in range(CH):
+            def scale_grad(s, planes):
+                if planes[0] == 0:
+                    hr = work.tile([P, CH, COLS], F32, bufs=3)
+                    state[s]["hr"] = hr
+                hr = state[s]["hr"]
+                for d in planes:
                     nc.vector.scalar_tensor_tensor(
                         out=hr[:, d, :],
                         in0=planes_g[s][:, d, :],
@@ -143,26 +143,42 @@ def tile_trianglemultiplicativeupdate_pa_v_kernel(
                         op0=ALU.mult,
                         op1=ALU.mult,
                     )
-                state[s]["hr"] = hr
 
             def add_up_hr(s):
-                sum_turned = work.tile([P, COLS], F32)
-                nc.scalar.copy(out=sum_turned[:], in_=turn_and_add(state[s]["hr"], CH)[:])
-                state[s]["sum_hr_turned"] = sum_turned
+                mean_turned = work.tile([P, COLS], F32)
+                nc.scalar.activation(out=mean_turned[:], in_=turn_and_add(state[s]["hr"], CH)[:], func=COPY, scale=1.0 / CH)
+                state[s]["mean_turned"] = mean_turned
 
-            def turn_back_hr(s):
-                state[s]["sum_hr"] = turn_back(state[s]["sum_hr_turned"])
+            def turn_back_mean(s):
+                mean_straight = sums.tile([P, COLS], F32, bufs=1)
+                for b in range(0, COLS, P):
+                    nc.tensor.transpose(
+                        out=mean_straight[:, b : b + P], in_=state[s]["mean_turned"][:, b : b + P], identity=identity[:]
+                    )
+                state[s]["mean_straight"] = mean_straight
 
-            def centre_x(s):
-                xc = state[s]["xc"]
-                nc.vector.tensor_tensor(out=xc[:], in0=xc[:], in1=over_planes(state[s]["mu_rstd"][:, 0, :], CH), op=ALU.subtract)
+            def multiply(s):
+                prod = work.tile([P, CH + 1, COLS], F32)
+                for lo in range(0, CH, HALF_CH):
+                    planes = slice(lo, lo + HALF_CH)
+                    nc.gpsimd.tensor_tensor(
+                        out=prod[:, planes, :], in0=state[s]["hr"][:, planes, :], in1=planes_x[s][:, planes, :], op=ALU.mult
+                    )
+                state[s]["prod"] = prod
 
             def correlate(s):
-                prod = work.tile([P, CH, COLS], F32)
-                nc.gpsimd.tensor_tensor(out=prod[:], in0=state[s]["hr"][:], in1=state[s]["xc"][:], op=ALU.mult)
-                state[s]["sum_prod_turned"] = turn_and_add(prod, CH)
+                prod = state[s]["prod"]
+                nc.vector.scalar_tensor_tensor(
+                    out=prod[:, CH, :],
+                    in0=state[s]["mean_straight"][:],
+                    scalar=-1.0 * CH,
+                    in1=state[s]["m"][:],
+                    op0=ALU.mult,
+                    op1=ALU.mult,
+                )
+                state[s]["sum_prod_turned"] = turn_and_add(prod, CH + 1)
 
-            def slope(s):
+            def slope_b(s):
                 kappa_turned = work.tile([P, COLS], F32)
                 nc.vector.scalar_tensor_tensor(
                     out=kappa_turned[:],
@@ -172,28 +188,52 @@ def tile_trianglemultiplicativeupdate_pa_v_kernel(
                     op0=ALU.mult,
                     op1=ALU.mult,
                 )
-                state[s]["kappa"] = turn_back(kappa_turned)
+                state[s]["kappa_turned"] = kappa_turned
+                kappa = sums.tile([P, COLS], F32, bufs=1)
+                for b in range(0, COLS, P):
+                    nc.tensor.transpose(out=kappa[:, b : b + P], in_=kappa_turned[:, b : b + P], identity=identity[:])
+                state[s]["kappa"] = kappa
+
+            def slope_c(s):
+                minus_kappa_mu = work.tile([P, COLS], F32)
+                nc.vector.scalar_tensor_tensor(
+                    out=minus_kappa_mu[:],
+                    in0=state[s]["kappa_turned"][:],
+                    scalar=-1.0,
+                    in1=state[s]["mu_rstd"][:, 0, :],
+                    op0=ALU.mult,
+                    op1=ALU.mult,
+                )
+                beta = sums.tile([P, COLS], F32, bufs=1)
+                state[s]["beta"] = beta
+                for b in range(0, COLS, P):
+                    for term, first_term in ((state[s]["mean_turned"], True), (minus_kappa_mu, False)):
+                        nc.tensor.matmul(
+                            out=beta[:, b : b + P],
+                            lhsT=term[:, b : b + P],
+                            rhs=identity[:],
+                            is_transpose=True,
+                            start=first_term,
+                            stop=not first_term,
+                        )
 
             def scale_xc(s):
                 for lo in range(0, CH, HALF_CH):
-                    part = state[s]["xc"][:, lo : lo + HALF_CH, :]
-                    nc.vector.tensor_tensor(out=part, in0=part, in1=over_planes(state[s]["kappa"][:], HALF_CH), op=ALU.mult)
+                    part = planes_x[s][:, lo : lo + HALF_CH, :]
+                    nc.vector.tensor_tensor(
+                        out=part, in0=part, in1=over_planes(state[s]["kappa"][:], HALF_CH), op=ALU.mult
+                    )
 
             def add_mean(s):
                 for lo in range(0, CH, HALF_CH):
-                    part = state[s]["xc"][:, lo : lo + HALF_CH, :]
-                    nc.vector.scalar_tensor_tensor(
-                        out=part,
-                        in0=over_planes(state[s]["sum_hr"][:], HALF_CH),
-                        scalar=1.0 / CH,
-                        in1=part,
-                        op0=ALU.mult,
-                        op1=ALU.add,
+                    part = planes_x[s][:, lo : lo + HALF_CH, :]
+                    nc.vector.tensor_tensor(
+                        out=part, in0=part, in1=over_planes(state[s]["beta"][:], HALF_CH), op=ALU.add
                     )
 
             def finish_dx(s, engine):
                 dx = work.tile([P, CH, COLS], BF16, align_bytes=64, bufs=1)
-                engine.tensor_tensor(out=dx[:], in0=state[s]["hr"][:], in1=state[s]["xc"][:], op=ALU.subtract)
+                engine.tensor_tensor(out=dx[:], in0=state[s]["hr"][:], in1=planes_x[s][:], op=ALU.subtract)
                 state[s]["dx"] = dx
 
             def quantise_dx(s):
@@ -210,30 +250,38 @@ def tile_trianglemultiplicativeupdate_pa_v_kernel(
                 nc.sync.dma_start(out=a_ld[:], in_=a_rows[:, :, kt * K_TILE : (kt + 1) * K_TILE, :])
                 a_tiles[kt] = a_ld
 
-            def lay_out_a(kt):
-                a_planes = work.tile([P, CH, K_TILE * PACK], BF16, align_bytes=64)
-                to_planes(a_planes, a_tiles[kt])
-                keep_ik = work.tile([P, K_TILE * PACK], BF16)
-                nc.scalar.copy(
-                    out=keep_ik[:].rearrange("p (k t) -> p k t", t=PACK),
-                    in_=mask_ik_sb[:, :, kt * K_TILE : (kt + 1) * K_TILE].rearrange("p t k -> p k t"),
-                )
-                a_tiles[kt] = (a_planes, keep_ik)
+            a_halves = {}
+            keeps = {}
 
-            def mask_a(kt):
-                a_planes, keep_ik = a_tiles[kt]
+            def lay_out_a(kt, lo):
+                if lo == 0:
+                    keep_ik = work.tile([P, K_TILE * PACK], BF16)
+                    nc.scalar.copy(
+                        out=keep_ik[:].rearrange("p (k t) -> p k t", t=PACK),
+                        in_=mask_ik_sb[:, :, kt * K_TILE : (kt + 1) * K_TILE].rearrange("p t k -> p k t"),
+                    )
+                    keeps[kt] = keep_ik
+                a_planes = work.tile([P, HALF_CH, K_TILE * PACK], BF16, align_bytes=64)
+                nc.scalar.copy(
+                    out=a_planes[:].rearrange("p d (c t) -> p c t d", t=PACK),
+                    in_=a_tiles[kt][:, :, :, lo : lo + HALF_CH].rearrange("p t c d -> p c t d"),
+                )
+                a_halves[(kt, lo)] = a_planes
+
+            def mask_a(kt, lo):
+                a_planes = a_halves[(kt, lo)]
                 nc.vector.tensor_tensor(
                     out=a_planes[:],
                     in0=a_planes[:],
-                    in1=keep_ik[:].unsqueeze(1).to_broadcast([P, CH, K_TILE * PACK]),
+                    in1=keeps[kt][:].unsqueeze(1).to_broadcast([P, HALF_CH, K_TILE * PACK]),
                     op=ALU.mult,
                 )
 
-            def quantise_a(kt):
+            def quantise_a(kt, lo):
                 nc.vector.quantize_mx(
-                    out=a_codes[:, kt, :, :].rearrange("p d k -> p (d k)").bitcast(E4M3_X4),
-                    scales=a_scales[:, kt, :, :].rearrange("p d k -> p (d k)"),
-                    in_=a_tiles[kt][0][:].rearrange("p d c -> p (d c)"),
+                    out=a_codes[:, kt, lo : lo + HALF_CH, :].rearrange("p d k -> p (d k)").bitcast(E4M3_X4),
+                    scales=a_scales[:, kt, lo : lo + HALF_CH, :].rearrange("p d k -> p (d k)"),
+                    in_=a_halves[(kt, lo)][:].rearrange("p d c -> p (d c)"),
                 )
 
             load(0)
@@ -257,29 +305,33 @@ def tile_trianglemultiplicativeupdate_pa_v_kernel(
                     finish_dx(third, nc.gpsimd if third < STEPS - 1 else nc.vector)
                 if first + 1 < STEPS:
                     lay_out_g(first + 1)
+                    lay_out_x(first + 1)
                 if first < STEPS:
-                    scale_grad(first)
+                    scale_grad(first, (0, 1, 2, 3, 4, 5))
                 if 0 <= second < STEPS:
-                    slope(second)
+                    slope_b(second)
+                if first < STEPS:
+                    scale_grad(first, (6, 7))
+                if 0 <= second < STEPS:
+                    slope_c(second)
                 if first < STEPS:
                     add_up_hr(first)
+                    turn_back_mean(first)
+                    multiply(first)
                 if first + 1 < STEPS:
                     lay_out_pairs(first + 1)
-                if first < STEPS:
-                    turn_back_hr(first)
-                    centre_x(first)
-                    correlate(first)
+                if kt < K_TILES:
+                    lay_out_a(kt, HALF_CH * (turn % 2))
                 if first + 1 < STEPS:
                     square_rstd(first + 1)
-                    lay_out_x(first + 1)
-                if turn % 2 == 0 and kt < K_TILES:
-                    lay_out_a(kt)
                 if 0 <= second < STEPS:
                     scale_xc(second)
                     add_mean(second)
-                if turn % 2 == 1 and kt < K_TILES:
-                    mask_a(kt)
-                    quantise_a(kt)
+                if first < STEPS:
+                    correlate(first)
+                if 1 <= turn <= 2 * K_TILES:
+                    mask_a((turn - 1) // 2, HALF_CH * ((turn - 1) % 2))
+                    quantise_a((turn - 1) // 2, HALF_CH * ((turn - 1) % 2))
                 if 0 <= third:
                     quantise_dx(third)
 

@@ -22,9 +22,24 @@ STEPS = SIDE // J_STEP
 COLS = J_STEP * PACK
 K_TILE = 128
 K_TILES = SIDE // K_TILE
+A_FIRST_TURN = 2
+PIECES = 2
+WB = 3
+PIECES_LAST = 2
+G_PLANES = 8
 
 FLOPS = 2 * CH * SIDE * SIDE * SIDE
 BYTES = SIDE * SIDE * (CH * (2 + 2 + 4 + 4) + 2 + 2 + 4 + 4) + 2 * CH
+
+
+def a_halves_laid_out_in(turn):
+    doubled = STEPS - 2
+    if A_FIRST_TURN <= turn < doubled:
+        return [turn - A_FIRST_TURN]
+    if doubled <= turn < STEPS:
+        first_half = doubled - A_FIRST_TURN + 2 * (turn - doubled)
+        return [first_half, first_half + 1]
+    return []
 
 
 def tile_trianglemultiplicativeupdate_pa_v_kernel(
@@ -41,9 +56,9 @@ def tile_trianglemultiplicativeupdate_pa_v_kernel(
     mask_kj_rows = mask_kj[0].rearrange("(kt p) j -> p kt j", p=P)
     out_rows = out[0].rearrange("(kt p) j d -> kt p (j d)", p=P)
 
-    def to_planes(planes, loaded):
+    def to_planes(planes, loaded, copy):
         for d in range(0, CH, HALF_CH):
-            nc.scalar.copy(
+            copy(
                 out=planes[:, d : d + HALF_CH, :].rearrange("p d (c t) -> p c t d", t=PACK),
                 in_=loaded[:, :, :, d : d + HALF_CH].rearrange("p t c d -> p c t d"),
             )
@@ -100,7 +115,7 @@ def tile_trianglemultiplicativeupdate_pa_v_kernel(
                         )
                 return turned
 
-            def lay_out_pairs(s):
+            def copy_pairs(s):
                 rstd_ld, g_ld, mu_ld, x_ld = loaded[s]
                 r = work.tile([P, 1, COLS], F32)
                 nc.scalar.copy(
@@ -108,11 +123,16 @@ def tile_trianglemultiplicativeupdate_pa_v_kernel(
                 )
                 m = work.tile([P, COLS], F32)
                 nc.scalar.copy(out=m[:].rearrange("p (j t) -> p j t", t=PACK), in_=mu_ld[:].rearrange("p t j -> p j t"))
+                state[s] = {"r": r, "m": m}
+
+            def stage_pairs(s):
+                r, m = state[s]["r"], state[s]["m"]
                 mu_rstd = sums.tile([P, 2, COLS], F32)
                 nc.tensor.matmul(out=mu_rstd[:, 1, :], lhsT=identity[:], rhs=r[:, 0, :], start=True, stop=True)
                 for b in range(0, COLS, P):
                     nc.tensor.transpose(out=mu_rstd[:, 0, b : b + P], in_=m[:, b : b + P], identity=identity[:])
-                state[s] = {"mu_rstd": mu_rstd, "m": m, "r_turned": turn_and_add(r, 1)}
+                state[s]["mu_rstd"] = mu_rstd
+                state[s]["r_turned"] = turn_and_add(r, 1)
 
             def square_rstd(s):
                 r_sq_turned = work.tile([P, COLS], F32, bufs=3)
@@ -121,12 +141,12 @@ def tile_trianglemultiplicativeupdate_pa_v_kernel(
 
             def lay_out_g(s):
                 g = work.tile([P, CH, COLS], BF16)
-                to_planes(g, loaded[s][1])
+                to_planes(g, loaded[s][1], nc.scalar.copy)
                 planes_g[s] = g
 
-            def lay_out_x(s):
+            def lay_out_x(s, copy):
                 xc = work.tile([P, CH, COLS], F32, bufs=4)
-                to_planes(xc, loaded[s][3])
+                to_planes(xc, loaded[s][3], copy)
                 planes_x[s] = xc
 
             def scale_grad(s, planes):
@@ -157,11 +177,11 @@ def tile_trianglemultiplicativeupdate_pa_v_kernel(
                     )
                 state[s]["mean_straight"] = mean_straight
 
-            def multiply(s):
+            def multiply(s, engine):
                 prod = work.tile([P, CH + 1, COLS], F32)
                 for lo in range(0, CH, HALF_CH):
                     planes = slice(lo, lo + HALF_CH)
-                    nc.gpsimd.tensor_tensor(
+                    engine.tensor_tensor(
                         out=prod[:, planes, :], in0=state[s]["hr"][:, planes, :], in1=planes_x[s][:, planes, :], op=ALU.mult
                     )
                 state[s]["prod"] = prod
@@ -231,10 +251,13 @@ def tile_trianglemultiplicativeupdate_pa_v_kernel(
                         out=part, in0=part, in1=over_planes(state[s]["beta"][:], HALF_CH), op=ALU.add
                     )
 
-            def finish_dx(s, engine):
-                dx = work.tile([P, CH, COLS], BF16, align_bytes=64, bufs=1)
-                engine.tensor_tensor(out=dx[:], in0=state[s]["hr"][:], in1=planes_x[s][:], op=ALU.subtract)
-                state[s]["dx"] = dx
+            def finish_dx(s, engine, planes):
+                if planes.start == 0:
+                    dx = work.tile([P, CH, COLS], BF16, align_bytes=64, bufs=1)
+                    state[s]["dx"] = dx
+                engine.tensor_tensor(
+                    out=state[s]["dx"][:, planes, :], in0=state[s]["hr"][:, planes, :], in1=planes_x[s][:, planes, :], op=ALU.subtract
+                )
 
             def quantise_dx(s):
                 cols = slice(s * J_STEP, (s + 1) * J_STEP)
@@ -288,24 +311,26 @@ def tile_trianglemultiplicativeupdate_pa_v_kernel(
             load(1)
             nc.sync.dma_start(out=mask_ik_sb[:], in_=mask_ik_rows)
             load_a(0)
-            lay_out_pairs(0)
+            copy_pairs(0)
+            stage_pairs(0)
             lay_out_g(0)
-            lay_out_x(0)
             square_rstd(0)
             for turn in range(STEPS + 2):
                 first, second, third = turn, turn - 1, turn - 2
-                kt = turn // 2
                 if turn + 2 < STEPS:
                     load(turn + 2)
-                if turn % 2 == 0 and kt + 1 < K_TILES:
-                    load_a(kt + 1)
+                for half_tile in a_halves_laid_out_in(turn + 1):
+                    if half_tile % 2 == 0 and half_tile > 0:
+                        load_a(half_tile // 2)
                 if turn == STEPS // 2:
                     nc.sync.dma_start(out=mask_kj_sb[:], in_=mask_kj_rows)
                 if 0 <= third:
-                    finish_dx(third, nc.gpsimd if third < STEPS - 1 else nc.vector)
+                    finish_dx(third, nc.gpsimd if third < STEPS - 1 else nc.vector, slice(0, G_PLANES))
                 if first + 1 < STEPS:
+                    copy_pairs(first + 1)
                     lay_out_g(first + 1)
-                    lay_out_x(first + 1)
+                    if turn > 0:
+                        lay_out_x(first + 1, nc.scalar.copy)
                 if first < STEPS:
                     scale_grad(first, (0, 1, 2, 3, 4, 5))
                 if 0 <= second < STEPS:
@@ -314,14 +339,19 @@ def tile_trianglemultiplicativeupdate_pa_v_kernel(
                     scale_grad(first, (6, 7))
                 if 0 <= second < STEPS:
                     slope_c(second)
+                if turn == 0:
+                    lay_out_x(0, nc.vector.tensor_copy)
                 if first < STEPS:
                     add_up_hr(first)
-                    turn_back_mean(first)
-                    multiply(first)
                 if first + 1 < STEPS:
-                    lay_out_pairs(first + 1)
-                if kt < K_TILES:
-                    lay_out_a(kt, HALF_CH * (turn % 2))
+                    stage_pairs(first + 1)
+                if first < STEPS:
+                    turn_back_mean(first)
+                    multiply(first, nc.gpsimd if turn > 0 else nc.vector)
+                if turn == 0:
+                    lay_out_x(1, nc.scalar.copy)
+                for half_tile in a_halves_laid_out_in(turn):
+                    lay_out_a(half_tile // 2, HALF_CH * (half_tile % 2))
                 if first + 1 < STEPS:
                     square_rstd(first + 1)
                 if 0 <= second < STEPS:
@@ -329,17 +359,19 @@ def tile_trianglemultiplicativeupdate_pa_v_kernel(
                     add_mean(second)
                 if first < STEPS:
                     correlate(first)
-                if 1 <= turn <= 2 * K_TILES:
-                    mask_a((turn - 1) // 2, HALF_CH * ((turn - 1) % 2))
-                    quantise_a((turn - 1) // 2, HALF_CH * ((turn - 1) % 2))
+                for half_tile in a_halves_laid_out_in(turn - 1):
+                    mask_a(half_tile // 2, HALF_CH * (half_tile % 2))
+                    quantise_a(half_tile // 2, HALF_CH * (half_tile % 2))
                 if 0 <= third:
+                    if G_PLANES < CH:
+                        finish_dx(third, nc.vector, slice(G_PLANES, CH))
                     quantise_dx(third)
 
         with tc.tile_pool(name="tail", bufs=2) as tail, tc.psum_pool(name="products", bufs=8) as products:
             for kt in range(K_TILES):
-                masked = tail.tile([P, CH, SIDE], F32)
-                woven_left = tail.tile([P, HALF_SIDE, CH], F32)
-                woven_right = tail.tile([P, HALF_SIDE, CH], F32)
+                pieces = PIECES_LAST if kt == K_TILES - 1 else PIECES
+                width = SIDE // pieces
+                banks = []
                 for d in range(CH):
                     product = products.tile([P, SIDE], F32)
                     nc.tensor.matmul_mx(
@@ -351,20 +383,30 @@ def tile_trianglemultiplicativeupdate_pa_v_kernel(
                         start=True,
                         stop=True,
                     )
-                    nc.vector.tensor_tensor(out=masked[:, d, :], in0=product[:], in1=mask_kj_sb[:, kt, :], op=ALU.mult)
-                    if d % HALF_CH == HALF_CH - 1:
-                        lo = d + 1 - HALF_CH
-                        nc.scalar.copy(
-                            out=woven_left[:, :, lo : lo + HALF_CH],
-                            in_=masked[:, lo : lo + HALF_CH, :HALF_SIDE].rearrange("p d j -> p j d"),
+                    banks.append(product)
+                for piece in range(pieces):
+                    lo_j = piece * width
+                    half = width // 2
+                    masked = tail.tile([P, CH, width], F32, tag="masked")
+                    woven_left = tail.tile([P, half, CH], F32, tag="woven_left", bufs=WB)
+                    woven_right = tail.tile([P, half, CH], F32, tag="woven_right", bufs=WB)
+                    for d in range(CH):
+                        nc.vector.tensor_tensor(
+                            out=masked[:, d, :], in0=banks[d][:, lo_j : lo_j + width], in1=mask_kj_sb[:, kt, lo_j : lo_j + width], op=ALU.mult
                         )
-                        nc.gpsimd.tensor_scalar(
-                            out=woven_right[:, :, lo : lo + HALF_CH],
-                            in0=masked[:, lo : lo + HALF_CH, HALF_SIDE:].rearrange("p d j -> p j d"),
-                            scalar1=1.0,
-                            scalar2=0.0,
-                            op0=ALU.mult,
-                            op1=ALU.add,
-                        )
-                nc.sync.dma_start(out=out_rows[kt][:, : HALF_SIDE * CH], in_=woven_left[:].rearrange("p j d -> p (j d)"))
-                nc.sync.dma_start(out=out_rows[kt][:, HALF_SIDE * CH :], in_=woven_right[:].rearrange("p j d -> p (j d)"))
+                        if d % HALF_CH == HALF_CH - 1:
+                            lo = d + 1 - HALF_CH
+                            nc.scalar.copy(
+                                out=woven_left[:, :, lo : lo + HALF_CH],
+                                in_=masked[:, lo : lo + HALF_CH, :half].rearrange("p d j -> p j d"),
+                            )
+                            nc.gpsimd.tensor_scalar(
+                                out=woven_right[:, :, lo : lo + HALF_CH],
+                                in0=masked[:, lo : lo + HALF_CH, half:].rearrange("p d j -> p j d"),
+                                scalar1=1.0,
+                                scalar2=0.0,
+                                op0=ALU.mult,
+                                op1=ALU.add,
+                            )
+                    nc.sync.dma_start(out=out_rows[kt][:, lo_j * CH : (lo_j + half) * CH], in_=woven_left[:].rearrange("p j d -> p (j d)"))
+                    nc.sync.dma_start(out=out_rows[kt][:, (lo_j + half) * CH : (lo_j + width) * CH], in_=woven_right[:].rearrange("p j d -> p (j d)"))

@@ -26,7 +26,7 @@ A_FIRST_TURN = 2
 PIECES = 2
 WB = 3
 PIECES_LAST = 2
-G_PLANES = 8
+G_PLANES = 6
 
 FLOPS = 2 * CH * SIDE * SIDE * SIDE
 BYTES = SIDE * SIDE * (CH * (2 + 2 + 4 + 4) + 2 + 2 + 4 + 4) + 2 * CH

@@ -26,7 +26,7 @@ A_FIRST_TURN = 2
 PIECES = 2
 WB = 3
 PIECES_LAST = 2
-G_PLANES = 6
+G_PLANES = 7
 
 FLOPS = 2 * CH * SIDE * SIDE * SIDE
 BYTES = SIDE * SIDE * (CH * (2 + 2 + 4 + 4) + 2 + 2 + 4 + 4) + 2 * CH
@@ -78,6 +78,8 @@ def tile_trianglemultiplicativeupdate_pa_v_kernel(
         ) as work, tc.psum_pool(name="sums", bufs=2) as sums:
             identity = once.tile([P, P], F32)
             make_identity(nc, identity[:])
+            identity_bf16 = once.tile([P, P], BF16)
+            make_identity(nc, identity_bf16[:])
             w_bf16 = once.tile([P, CH], BF16)
             nc.sync.dma_start(out=w_bf16[:], in_=ln_out_w.partition_broadcast(P))
             w = once.tile([P, CH], F32)
@@ -101,8 +103,7 @@ def tile_trianglemultiplicativeupdate_pa_v_kernel(
                 nc.sync.dma_start(out=x_ld[:], in_=x_rows[:, :, cols, :])
                 loaded[s] = (rstd_ld, g_ld, mu_ld, x_ld)
 
-            def turn_and_add(planes, count):
-                turned = sums.tile([P, COLS], F32, bufs=3)
+            def turn_and_add(planes, count, turned):
                 for b in range(0, COLS, P):
                     for d in range(count):
                         nc.tensor.matmul(
@@ -113,7 +114,14 @@ def tile_trianglemultiplicativeupdate_pa_v_kernel(
                             start=(d == 0),
                             stop=(d == count - 1),
                         )
-                return turned
+
+            hr_r_banks = {}
+
+            def hr_r_bank(turn_no):
+                if turn_no not in hr_r_banks:
+                    hr_r = sums.tile([P, 2, COLS], F32, bufs=1)
+                    hr_r_banks[turn_no] = hr_r
+                return hr_r_banks[turn_no]
 
             def copy_pairs(s):
                 rstd_ld, g_ld, mu_ld, x_ld = loaded[s]
@@ -132,11 +140,12 @@ def tile_trianglemultiplicativeupdate_pa_v_kernel(
                 for b in range(0, COLS, P):
                     nc.tensor.transpose(out=mu_rstd[:, 0, b : b + P], in_=m[:, b : b + P], identity=identity[:])
                 state[s]["mu_rstd"] = mu_rstd
-                state[s]["r_turned"] = turn_and_add(r, 1)
+                state[s]["r_turned"] = hr_r_bank(s - 1)[:, 1, :]
+                turn_and_add(r, 1, state[s]["r_turned"])
 
             def square_rstd(s):
                 r_sq_turned = work.tile([P, COLS], F32, bufs=3)
-                nc.scalar.activation(out=r_sq_turned[:], in_=state[s]["r_turned"][:], func=SQUARE)
+                nc.scalar.activation(out=r_sq_turned[:], in_=state[s]["r_turned"], func=SQUARE)
                 state[s]["r_sq_turned"] = r_sq_turned
 
             def lay_out_g(s):
@@ -166,16 +175,17 @@ def tile_trianglemultiplicativeupdate_pa_v_kernel(
 
             def add_up_hr(s):
                 mean_turned = work.tile([P, COLS], F32)
-                nc.scalar.activation(out=mean_turned[:], in_=turn_and_add(state[s]["hr"], CH)[:], func=COPY, scale=1.0 / CH)
+                turn_and_add(state[s]["hr"], CH, hr_r_bank(s)[:, 0, :])
+                nc.scalar.activation(out=mean_turned[:], in_=hr_r_bank(s)[:, 0, :], func=COPY, scale=1.0 / CH)
                 state[s]["mean_turned"] = mean_turned
 
             def turn_back_mean(s):
-                mean_straight = sums.tile([P, COLS], F32, bufs=1)
+                mean_prod = sums.tile([P, 2, COLS], F32, bufs=1)
                 for b in range(0, COLS, P):
                     nc.tensor.transpose(
-                        out=mean_straight[:, b : b + P], in_=state[s]["mean_turned"][:, b : b + P], identity=identity[:]
+                        out=mean_prod[:, 0, b : b + P], in_=state[s]["mean_turned"][:, b : b + P], identity=identity[:]
                     )
-                state[s]["mean_straight"] = mean_straight
+                state[s]["mean_prod"] = mean_prod
 
             def multiply(s, engine):
                 prod = work.tile([P, CH + 1, COLS], F32)
@@ -190,19 +200,19 @@ def tile_trianglemultiplicativeupdate_pa_v_kernel(
                 prod = state[s]["prod"]
                 nc.vector.scalar_tensor_tensor(
                     out=prod[:, CH, :],
-                    in0=state[s]["mean_straight"][:],
+                    in0=state[s]["mean_prod"][:, 0, :],
                     scalar=-1.0 * CH,
                     in1=state[s]["m"][:],
                     op0=ALU.mult,
                     op1=ALU.mult,
                 )
-                state[s]["sum_prod_turned"] = turn_and_add(prod, CH + 1)
+                turn_and_add(prod, CH + 1, state[s]["mean_prod"][:, 1, :])
 
             def slope_b(s):
                 kappa_turned = work.tile([P, COLS], F32)
                 nc.vector.scalar_tensor_tensor(
                     out=kappa_turned[:],
-                    in0=state[s]["sum_prod_turned"][:],
+                    in0=state[s]["mean_prod"][:, 1, :],
                     scalar=1.0 / CH,
                     in1=state[s]["r_sq_turned"][:],
                     op0=ALU.mult,
@@ -283,7 +293,9 @@ def tile_trianglemultiplicativeupdate_pa_v_kernel(
                         out=keep_ik[:].rearrange("p (k t) -> p k t", t=PACK),
                         in_=mask_ik_sb[:, :, kt * K_TILE : (kt + 1) * K_TILE].rearrange("p t k -> p k t"),
                     )
-                    keeps[kt] = keep_ik
+                    keep_ps = sums.tile([P, K_TILE * PACK], BF16)
+                    nc.tensor.matmul(out=keep_ps[:], lhsT=identity_bf16[:], rhs=keep_ik[:], start=True, stop=True)
+                    keeps[kt] = keep_ps
                 a_planes = work.tile([P, HALF_CH, K_TILE * PACK], BF16, align_bytes=64)
                 nc.scalar.copy(
                     out=a_planes[:].rearrange("p d (c t) -> p c t d", t=PACK),
@@ -341,11 +353,10 @@ def tile_trianglemultiplicativeupdate_pa_v_kernel(
                     slope_c(second)
                 if turn == 0:
                     lay_out_x(0, nc.vector.tensor_copy)
-                if first < STEPS:
-                    add_up_hr(first)
                 if first + 1 < STEPS:
                     stage_pairs(first + 1)
                 if first < STEPS:
+                    add_up_hr(first)
                     turn_back_mean(first)
                     multiply(first, nc.gpsimd if turn > 0 else nc.vector)
                 if turn == 0:
@@ -357,10 +368,11 @@ def tile_trianglemultiplicativeupdate_pa_v_kernel(
                 if 0 <= second < STEPS:
                     scale_xc(second)
                     add_mean(second)
+                for half_tile in a_halves_laid_out_in(turn - 1):
+                    mask_a(half_tile // 2, HALF_CH * (half_tile % 2))
                 if first < STEPS:
                     correlate(first)
                 for half_tile in a_halves_laid_out_in(turn - 1):
-                    mask_a(half_tile // 2, HALF_CH * (half_tile % 2))
                     quantise_a(half_tile // 2, HALF_CH * (half_tile % 2))
                 if 0 <= third:
                     if G_PLANES < CH:

@@ -351,6 +351,8 @@ def tile_trianglemultiplicativeupdate_pa_v_kernel(
                     scale_grad(first, (6, 7))
                 if 0 <= second < STEPS:
                     slope_c(second)
+                for half_tile in a_halves_laid_out_in(turn - 1):
+                    mask_a(half_tile // 2, HALF_CH * (half_tile % 2))
                 if turn == 0:
                     lay_out_x(0, nc.vector.tensor_copy)
                 if first + 1 < STEPS:
@@ -368,8 +370,6 @@ def tile_trianglemultiplicativeupdate_pa_v_kernel(
                 if 0 <= second < STEPS:
                     scale_xc(second)
                     add_mean(second)
-                for half_tile in a_halves_laid_out_in(turn - 1):
-                    mask_a(half_tile // 2, HALF_CH * (half_tile % 2))
                 if first < STEPS:
                     correlate(first)
                 for half_tile in a_halves_laid_out_in(turn - 1):

@@ -80,10 +80,15 @@ def tile_trianglemultiplicativeupdate_pa_v_kernel(
             make_identity(nc, identity[:])
             identity_bf16 = once.tile([P, P], BF16)
             make_identity(nc, identity_bf16[:])
-            w_bf16 = once.tile([P, CH], BF16)
-            nc.sync.dma_start(out=w_bf16[:], in_=ln_out_w.partition_broadcast(P))
+            w_row = once.tile([P, CH], BF16)
+            nc.vector.memset(w_row[:], 0.0)
+            nc.scalar.dma_start(out=w_row[0:1, :], in_=ln_out_w.partition_broadcast(1))
+            ones = once.tile([P, P], BF16)
+            nc.vector.memset(ones[:], 1.0)
+            w_spread = sums.tile([P, CH], F32, tag="kappa", bufs=1)
+            nc.tensor.matmul(out=w_spread[:], lhsT=ones[:], rhs=w_row[:], start=True, stop=True)
             w = once.tile([P, CH], F32)
-            nc.vector.tensor_copy(out=w[:], in_=w_bf16[:])
+            nc.vector.tensor_copy(out=w[:], in_=w_spread[:])
             mask_ik_sb = once.tile([P, PACK, SIDE], BF16)
 
             loaded = {}

@@ -26,7 +26,7 @@ A_FIRST_TURN = 2
 PIECES = 2
 WB = 3
 PIECES_LAST = 2
-G_PLANES = 7
+G_PLANES = 8
 
 FLOPS = 2 * CH * SIDE * SIDE * SIDE
 BYTES = SIDE * SIDE * (CH * (2 + 2 + 4 + 4) + 2 + 2 + 4 + 4) + 2 * CH
@@ -194,11 +194,7 @@ def tile_trianglemultiplicativeupdate_pa_v_kernel(
 
             def multiply(s, engine):
                 prod = work.tile([P, CH + 1, COLS], F32)
-                for lo in range(0, CH, HALF_CH):
-                    planes = slice(lo, lo + HALF_CH)
-                    engine.tensor_tensor(
-                        out=prod[:, planes, :], in0=state[s]["hr"][:, planes, :], in1=planes_x[s][:, planes, :], op=ALU.mult
-                    )
+                engine.tensor_tensor(out=prod[:, :CH, :], in0=state[s]["hr"][:], in1=planes_x[s][:], op=ALU.mult)
                 state[s]["prod"] = prod
 
             def correlate(s):

@@ -22,24 +22,21 @@ STEPS = SIDE // J_STEP
 COLS = J_STEP * PACK
 K_TILE = 128
 K_TILES = SIDE // K_TILE
-A_FIRST_TURN = 2
-PIECES = 2
-WB = 3
-PIECES_LAST = 2
-G_PLANES = 8
+J_BLOCK = SIDE // HALF_CH
+BLOCKS = SIDE // J_BLOCK
+STEPS_A_BLOCK = J_BLOCK // J_STEP
+A_FIRST_TURN = 1
+A_HALVES_A_TURN = 2
+PRODUCTS_A_TURN = 4
+PRODUCTS_A_DRAIN_TURN = 6
 
 FLOPS = 2 * CH * SIDE * SIDE * SIDE
 BYTES = SIDE * SIDE * (CH * (2 + 2 + 4 + 4) + 2 + 2 + 4 + 4) + 2 * CH
 
 
 def a_halves_laid_out_in(turn):
-    doubled = STEPS - 2
-    if A_FIRST_TURN <= turn < doubled:
-        return [turn - A_FIRST_TURN]
-    if doubled <= turn < STEPS:
-        first_half = doubled - A_FIRST_TURN + 2 * (turn - doubled)
-        return [first_half, first_half + 1]
-    return []
+    first_half = A_HALVES_A_TURN * (turn - A_FIRST_TURN)
+    return [half for half in range(first_half, first_half + A_HALVES_A_TURN) if 0 <= half < 2 * K_TILES]
 
 
 def tile_trianglemultiplicativeupdate_pa_v_kernel(
@@ -69,13 +66,17 @@ def tile_trianglemultiplicativeupdate_pa_v_kernel(
     with tc.manual_schedule(), tc.tile_pool(name="keep", bufs=1) as keep:
         a_codes = keep.tile([P, K_TILES, CH, K_TILE], U32, align_bytes=64)
         a_scales = keep.tile([P, K_TILES, CH, K_TILE], U8, align_bytes=64)
-        dx_codes = keep.tile([P, CH, SIDE], U32, align_bytes=64)
-        dx_scales = keep.tile([P, CH, SIDE], U8, align_bytes=64)
+        even_codes = keep.tile([P, CH, HALF_CH, J_BLOCK], U32, align_bytes=64)
+        even_scales = keep.tile([P, CH, HALF_CH, J_BLOCK], U8, align_bytes=64)
+        odd_codes = keep.tile([P, CH, HALF_CH, J_BLOCK], U32, align_bytes=64)
+        odd_scales = keep.tile([P, CH, HALF_CH, J_BLOCK], U8, align_bytes=64)
+        dx_codes = (even_codes, odd_codes)
+        dx_scales = (even_scales, odd_scales)
         mask_kj_sb = keep.tile([P, K_TILES, SIDE], BF16)
 
         with tc.tile_pool(name="once", bufs=1) as once, tc.tile_pool(name="loads", bufs=2) as loads, tc.tile_pool(
             name="work", bufs=2
-        ) as work, tc.psum_pool(name="sums", bufs=2) as sums:
+        ) as work, tc.tile_pool(name="stores", bufs=4) as stores, tc.psum_pool(name="sums", bufs=1) as sums:
             identity = once.tile([P, P], F32)
             make_identity(nc, identity[:])
             identity_bf16 = once.tile([P, P], BF16)
@@ -85,11 +86,14 @@ def tile_trianglemultiplicativeupdate_pa_v_kernel(
             nc.scalar.dma_start(out=w_row[0:1, :], in_=ln_out_w.partition_broadcast(1))
             ones = once.tile([P, P], BF16)
             nc.vector.memset(ones[:], 1.0)
-            w_spread = sums.tile([P, CH], F32, tag="kappa", bufs=1)
+            w_spread = sums.tile([P, CH], F32, tag="kappa_beta")
             nc.tensor.matmul(out=w_spread[:], lhsT=ones[:], rhs=w_row[:], start=True, stop=True)
             w = once.tile([P, CH], F32)
             nc.vector.tensor_copy(out=w[:], in_=w_spread[:])
             mask_ik_sb = once.tile([P, PACK, SIDE], BF16)
+            for parity in range(2):
+                nc.vector.memset(dx_codes[parity][:], 0)
+                nc.vector.memset(dx_scales[parity][:].rearrange("p d s j -> p (d s j)").bitcast(U32), 0)
 
             loaded = {}
             planes_g = {}
@@ -124,7 +128,7 @@ def tile_trianglemultiplicativeupdate_pa_v_kernel(
 
             def hr_r_bank(turn_no):
                 if turn_no not in hr_r_banks:
-                    hr_r = sums.tile([P, 2, COLS], F32, bufs=1)
+                    hr_r = sums.tile([P, 2, COLS], F32)
                     hr_r_banks[turn_no] = hr_r
                 return hr_r_banks[turn_no]
 
@@ -138,18 +142,24 @@ def tile_trianglemultiplicativeupdate_pa_v_kernel(
                 nc.scalar.copy(out=m[:].rearrange("p (j t) -> p j t", t=PACK), in_=mu_ld[:].rearrange("p t j -> p j t"))
                 state[s] = {"r": r, "m": m}
 
+            def stage_rstd(s, mu_rstd):
+                nc.tensor.matmul(out=mu_rstd[:, 1, :], lhsT=identity[:], rhs=state[s]["r"][:, 0, :], start=True, stop=True)
+                state[s]["rstd"] = mu_rstd[:, 1, :]
+
             def stage_pairs(s):
-                r, m = state[s]["r"], state[s]["m"]
                 mu_rstd = sums.tile([P, 2, COLS], F32)
-                nc.tensor.matmul(out=mu_rstd[:, 1, :], lhsT=identity[:], rhs=r[:, 0, :], start=True, stop=True)
+                if s + 1 < STEPS:
+                    stage_rstd(s + 1, mu_rstd)
                 for b in range(0, COLS, P):
-                    nc.tensor.transpose(out=mu_rstd[:, 0, b : b + P], in_=m[:, b : b + P], identity=identity[:])
-                state[s]["mu_rstd"] = mu_rstd
-                state[s]["r_turned"] = hr_r_bank(s - 1)[:, 1, :]
-                turn_and_add(r, 1, state[s]["r_turned"])
+                    nc.tensor.transpose(
+                        out=mu_rstd[:, 0, b : b + P], in_=state[s]["m"][:, b : b + P], identity=identity[:]
+                    )
+                state[s]["mu_turned"] = mu_rstd[:, 0, :]
+                state[s]["r_turned"] = hr_r_bank(s)[:, 1, :]
+                turn_and_add(state[s]["r"], 1, state[s]["r_turned"])
 
             def square_rstd(s):
-                r_sq_turned = work.tile([P, COLS], F32, bufs=3)
+                r_sq_turned = work.tile([P, COLS], F32)
                 nc.scalar.activation(out=r_sq_turned[:], in_=state[s]["r_turned"], func=SQUARE)
                 state[s]["r_sq_turned"] = r_sq_turned
 
@@ -173,7 +183,7 @@ def tile_trianglemultiplicativeupdate_pa_v_kernel(
                         out=hr[:, d, :],
                         in0=planes_g[s][:, d, :],
                         scalar=w[:, d : d + 1],
-                        in1=state[s]["mu_rstd"][:, 1, :],
+                        in1=state[s]["rstd"],
                         op0=ALU.mult,
                         op1=ALU.mult,
                     )
@@ -185,7 +195,7 @@ def tile_trianglemultiplicativeupdate_pa_v_kernel(
                 state[s]["mean_turned"] = mean_turned
 
             def turn_back_mean(s):
-                mean_prod = sums.tile([P, 2, COLS], F32, bufs=1)
+                mean_prod = sums.tile([P, 2, COLS], F32)
                 for b in range(0, COLS, P):
                     nc.tensor.transpose(
                         out=mean_prod[:, 0, b : b + P], in_=state[s]["mean_turned"][:, b : b + P], identity=identity[:]
@@ -193,7 +203,7 @@ def tile_trianglemultiplicativeupdate_pa_v_kernel(
                 state[s]["mean_prod"] = mean_prod
 
             def multiply(s, engine):
-                prod = work.tile([P, CH + 1, COLS], F32)
+                prod = work.tile([P, CH + 1, COLS], F32, bufs=1)
                 engine.tensor_tensor(out=prod[:, :CH, :], in0=state[s]["hr"][:], in1=planes_x[s][:], op=ALU.mult)
                 state[s]["prod"] = prod
 
@@ -220,10 +230,12 @@ def tile_trianglemultiplicativeupdate_pa_v_kernel(
                     op1=ALU.mult,
                 )
                 state[s]["kappa_turned"] = kappa_turned
-                kappa = sums.tile([P, COLS], F32, bufs=1)
+                kappa_beta = sums.tile([P, 2, COLS], F32)
                 for b in range(0, COLS, P):
-                    nc.tensor.transpose(out=kappa[:, b : b + P], in_=kappa_turned[:, b : b + P], identity=identity[:])
-                state[s]["kappa"] = kappa
+                    nc.tensor.transpose(
+                        out=kappa_beta[:, 0, b : b + P], in_=kappa_turned[:, b : b + P], identity=identity[:]
+                    )
+                state[s]["kappa_beta"] = kappa_beta
 
             def slope_c(s):
                 minus_kappa_mu = work.tile([P, COLS], F32)
@@ -231,16 +243,14 @@ def tile_trianglemultiplicativeupdate_pa_v_kernel(
                     out=minus_kappa_mu[:],
                     in0=state[s]["kappa_turned"][:],
                     scalar=-1.0,
-                    in1=state[s]["mu_rstd"][:, 0, :],
+                    in1=state[s]["mu_turned"],
                     op0=ALU.mult,
                     op1=ALU.mult,
                 )
-                beta = sums.tile([P, COLS], F32, bufs=1)
-                state[s]["beta"] = beta
                 for b in range(0, COLS, P):
                     for term, first_term in ((state[s]["mean_turned"], True), (minus_kappa_mu, False)):
                         nc.tensor.matmul(
-                            out=beta[:, b : b + P],
+                            out=state[s]["kappa_beta"][:, 1, b : b + P],
                             lhsT=term[:, b : b + P],
                             rhs=identity[:],
                             is_transpose=True,
@@ -252,14 +262,14 @@ def tile_trianglemultiplicativeupdate_pa_v_kernel(
                 for lo in range(0, CH, HALF_CH):
                     part = planes_x[s][:, lo : lo + HALF_CH, :]
                     nc.vector.tensor_tensor(
-                        out=part, in0=part, in1=over_planes(state[s]["kappa"][:], HALF_CH), op=ALU.mult
+                        out=part, in0=part, in1=over_planes(state[s]["kappa_beta"][:, 0, :], HALF_CH), op=ALU.mult
                     )
 
             def add_mean(s):
                 for lo in range(0, CH, HALF_CH):
                     part = planes_x[s][:, lo : lo + HALF_CH, :]
                     nc.vector.tensor_tensor(
-                        out=part, in0=part, in1=over_planes(state[s]["beta"][:], HALF_CH), op=ALU.add
+                        out=part, in0=part, in1=over_planes(state[s]["kappa_beta"][:, 1, :], HALF_CH), op=ALU.add
                     )
 
             def finish_dx(s, engine, planes):
@@ -270,11 +280,50 @@ def tile_trianglemultiplicativeupdate_pa_v_kernel(
                     out=state[s]["dx"][:, planes, :], in0=state[s]["hr"][:, planes, :], in1=planes_x[s][:, planes, :], op=ALU.subtract
                 )
 
-            def quantise_dx(s):
-                cols = slice(s * J_STEP, (s + 1) * J_STEP)
-                for d in range(CH):
+            def quantise_dx(s, planes):
+                block, part = divmod(s, STEPS_A_BLOCK)
+                cols = slice(part * J_STEP, (part + 1) * J_STEP)
+                for d in planes:
                     nc.vector.quantize_mx(
-                        out=dx_codes[:, d, cols].bitcast(E5M2_X4), scales=dx_scales[:, d, cols], in_=state[s]["dx"][:, d, :]
+                        out=dx_codes[block % 2][:, d, d % HALF_CH, cols].bitcast(E5M2_X4),
+                        scales=dx_scales[block % 2][:, d, d % HALF_CH, cols],
+                        in_=state[s]["dx"][:, d, :],
+                    )
+
+            products = {}
+            woven_tiles = {}
+
+            def multiply_mx(block, kt, lo):
+                product = sums.tile([P, SIDE], F32, bufs=3)
+                for q in range(HALF_CH):
+                    d = lo + q
+                    nc.tensor.matmul_mx(
+                        out=product[:],
+                        lhsT=a_codes[:, kt, d, :].bitcast(E4M3_X4),
+                        lhsT_scale=a_scales[:, kt, d, :],
+                        rhs=dx_codes[block % 2][:, d, :, :].rearrange("p s j -> p (s j)").bitcast(E5M2_X4),
+                        rhs_scale=dx_scales[block % 2][:, d, :, :].rearrange("p s j -> p (s j)"),
+                        start=(q == 0),
+                        stop=(q == HALF_CH - 1),
+                    )
+                products[(block, kt, lo)] = product
+
+            def mask_and_store(block, kt, lo):
+                if lo == 0:
+                    woven = stores.tile([P, J_BLOCK, CH], F32)
+                    woven_tiles[(block, kt)] = woven
+                woven = woven_tiles[(block, kt)]
+                cols = slice(block * J_BLOCK, (block + 1) * J_BLOCK)
+                nc.vector.tensor_tensor(
+                    out=woven[:, :, lo : lo + HALF_CH],
+                    in0=products[(block, kt, lo)][:].rearrange("p (d j) -> p j d", d=HALF_CH),
+                    in1=mask_kj_sb[:, kt, cols].unsqueeze(2).to_broadcast([P, J_BLOCK, HALF_CH]),
+                    op=ALU.mult,
+                )
+                if lo > 0:
+                    nc.sync.dma_start(
+                        out=out_rows[kt][:, block * J_BLOCK * CH : (block + 1) * J_BLOCK * CH],
+                        in_=woven[:].rearrange("p j d -> p (j d)"),
                     )
 
             a_tiles = {}
@@ -289,7 +338,7 @@ def tile_trianglemultiplicativeupdate_pa_v_kernel(
 
             def lay_out_a(kt, lo):
                 if lo == 0:
-                    keep_ik = work.tile([P, K_TILE * PACK], BF16)
+                    keep_ik = work.tile([P, K_TILE * PACK], BF16, bufs=1)
                     nc.scalar.copy(
                         out=keep_ik[:].rearrange("p (k t) -> p k t", t=PACK),
                         in_=mask_ik_sb[:, :, kt * K_TILE : (kt + 1) * K_TILE].rearrange("p t k -> p k t"),
@@ -297,7 +346,7 @@ def tile_trianglemultiplicativeupdate_pa_v_kernel(
                     keep_ps = sums.tile([P, K_TILE * PACK], BF16)
                     nc.tensor.matmul(out=keep_ps[:], lhsT=identity_bf16[:], rhs=keep_ik[:], start=True, stop=True)
                     keeps[kt] = keep_ps
-                a_planes = work.tile([P, HALF_CH, K_TILE * PACK], BF16, align_bytes=64)
+                a_planes = work.tile([P, HALF_CH, K_TILE * PACK], BF16, align_bytes=64, bufs=4)
                 nc.scalar.copy(
                     out=a_planes[:].rearrange("p d (c t) -> p c t d", t=PACK),
                     in_=a_tiles[kt][:, :, :, lo : lo + HALF_CH].rearrange("p t c d -> p c t d"),
@@ -320,30 +369,69 @@ def tile_trianglemultiplicativeupdate_pa_v_kernel(
                     in_=a_halves[(kt, lo)][:].rearrange("p d c -> p (d c)"),
                 )
 
+            waiting = [
+                (block, kt, lo) for block in range(BLOCKS) for kt in range(K_TILES) for lo in range(0, CH, HALF_CH)
+            ]
+
+            def products_of(turn):
+                most = PRODUCTS_A_TURN if turn < STEPS else PRODUCTS_A_DRAIN_TURN
+                chosen = []
+                while waiting and len(chosen) < most:
+                    block, kt, lo = waiting[0]
+                    dx_turn = (block + 1) * STEPS_A_BLOCK - 1 + 2
+                    a_turn = A_FIRST_TURN + (2 * kt + 1) // A_HALVES_A_TURN + 1
+                    if max(dx_turn, a_turn) >= turn:
+                        break
+                    chosen.append(waiting[0])
+                    waiting.remove(waiting[0])
+                return chosen
+
             load(0)
             load(1)
             nc.sync.dma_start(out=mask_ik_sb[:], in_=mask_ik_rows)
             load_a(0)
             copy_pairs(0)
-            stage_pairs(0)
+            first_rstd = sums.tile([P, 2, COLS], F32, tag="mu_rstd")
+            stage_rstd(0, first_rstd)
             lay_out_g(0)
-            square_rstd(0)
             for turn in range(STEPS + 2):
                 first, second, third = turn, turn - 1, turn - 2
+                to_fill = products_of(turn)
+                to_empty = list(to_fill)
+
+                def fill(count):
+                    for i in range(min(count, len(to_fill))):
+                        bank = to_fill[0]
+                        to_fill.remove(bank)
+                        multiply_mx(*bank)
+
+                def empty(count):
+                    for i in range(min(count, len(to_empty))):
+                        bank = to_empty[0]
+                        to_empty.remove(bank)
+                        mask_and_store(*bank)
+
                 if turn + 2 < STEPS:
                     load(turn + 2)
                 for half_tile in a_halves_laid_out_in(turn + 1):
                     if half_tile % 2 == 0 and half_tile > 0:
                         load_a(half_tile // 2)
-                if turn == STEPS // 2:
+                if turn == 2:
                     nc.sync.dma_start(out=mask_kj_sb[:], in_=mask_kj_rows)
-                if 0 <= third:
-                    finish_dx(third, nc.gpsimd if third < STEPS - 1 else nc.vector, slice(0, G_PLANES))
+                if 0 <= third < STEPS - 1:
+                    finish_dx(third, nc.gpsimd, slice(0, CH))
                 if first + 1 < STEPS:
                     copy_pairs(first + 1)
                     lay_out_g(first + 1)
                     if turn > 0:
                         lay_out_x(first + 1, nc.scalar.copy)
+                fill(1)
+                if third == STEPS - 1:
+                    for lo in range(0, CH, HALF_CH):
+                        finish_dx(third, nc.vector, slice(lo, lo + HALF_CH))
+                        fill(1)
+                        empty(1)
+                        quantise_dx(third, range(lo, lo + HALF_CH))
                 if first < STEPS:
                     scale_grad(first, (0, 1, 2, 3, 4, 5))
                 if 0 <= second < STEPS:
@@ -352,74 +440,39 @@ def tile_trianglemultiplicativeupdate_pa_v_kernel(
                     scale_grad(first, (6, 7))
                 if 0 <= second < STEPS:
                     slope_c(second)
+                if first < STEPS:
+                    add_up_hr(first)
+                fill(1)
+                empty(1)
                 for half_tile in a_halves_laid_out_in(turn - 1):
                     mask_a(half_tile // 2, HALF_CH * (half_tile % 2))
                 if turn == 0:
                     lay_out_x(0, nc.vector.tensor_copy)
-                if first + 1 < STEPS:
-                    stage_pairs(first + 1)
                 if first < STEPS:
-                    add_up_hr(first)
                     turn_back_mean(first)
+                    stage_pairs(first)
                     multiply(first, nc.gpsimd if turn > 0 else nc.vector)
                 if turn == 0:
                     lay_out_x(1, nc.scalar.copy)
+                fill(2)
                 for half_tile in a_halves_laid_out_in(turn):
                     lay_out_a(half_tile // 2, HALF_CH * (half_tile % 2))
-                if first + 1 < STEPS:
-                    square_rstd(first + 1)
+                if first < STEPS:
+                    square_rstd(first)
                 if 0 <= second < STEPS:
                     scale_xc(second)
+                    empty(1)
                     add_mean(second)
                 if first < STEPS:
                     correlate(first)
+                empty(1)
                 for half_tile in a_halves_laid_out_in(turn - 1):
                     quantise_a(half_tile // 2, HALF_CH * (half_tile % 2))
-                if 0 <= third:
-                    if G_PLANES < CH:
-                        finish_dx(third, nc.vector, slice(G_PLANES, CH))
-                    quantise_dx(third)
+                if 0 <= third < STEPS - 1:
+                    quantise_dx(third, range(CH))
+                fill(PRODUCTS_A_DRAIN_TURN)
+                empty(PRODUCTS_A_DRAIN_TURN)
 
-        with tc.tile_pool(name="tail", bufs=2) as tail, tc.psum_pool(name="products", bufs=8) as products:
-            for kt in range(K_TILES):
-                pieces = PIECES_LAST if kt == K_TILES - 1 else PIECES
-                width = SIDE // pieces
-                banks = []
-                for d in range(CH):
-                    product = products.tile([P, SIDE], F32)
-                    nc.tensor.matmul_mx(
-                        out=product[:],
-                        lhsT=a_codes[:, kt, d, :].bitcast(E4M3_X4),
-                        lhsT_scale=a_scales[:, kt, d, :],
-                        rhs=dx_codes[:, d, :].bitcast(E5M2_X4),
-                        rhs_scale=dx_scales[:, d, :],
-                        start=True,
-                        stop=True,
-                    )
-                    banks.append(product)
-                for piece in range(pieces):
-                    lo_j = piece * width
-                    half = width // 2
-                    masked = tail.tile([P, CH, width], F32, tag="masked")
-                    woven_left = tail.tile([P, half, CH], F32, tag="woven_left", bufs=WB)
-                    woven_right = tail.tile([P, half, CH], F32, tag="woven_right", bufs=WB)
-                    for d in range(CH):
-                        nc.vector.tensor_tensor(
-                            out=masked[:, d, :], in0=banks[d][:, lo_j : lo_j + width], in1=mask_kj_sb[:, kt, lo_j : lo_j + width], op=ALU.mult
-                        )
-                        if d % HALF_CH == HALF_CH - 1:
-                            lo = d + 1 - HALF_CH
-                            nc.scalar.copy(
-                                out=woven_left[:, :, lo : lo + HALF_CH],
-                                in_=masked[:, lo : lo + HALF_CH, :half].rearrange("p d j -> p j d"),
-                            )
-                            nc.gpsimd.tensor_scalar(
-                                out=woven_right[:, :, lo : lo + HALF_CH],
-                                in0=masked[:, lo : lo + HALF_CH, half:].rearrange("p d j -> p j d"),
-                                scalar1=1.0,
-                                scalar2=0.0,
-                                op0=ALU.mult,
-                                op1=ALU.add,
-                            )
-                    nc.sync.dma_start(out=out_rows[kt][:, lo_j * CH : (lo_j + half) * CH], in_=woven_left[:].rearrange("p j d -> p (j d)"))
-                    nc.sync.dma_start(out=out_rows[kt][:, (lo_j + half) * CH : (lo_j + width) * CH], in_=woven_right[:].rearrange("p j d -> p (j d)"))
+            for bank in sorted(waiting, key=lambda bank: (bank[0], bank[2], bank[1])):
+                multiply_mx(*bank)
+                mask_and_store(*bank)

@@ -27,8 +27,8 @@ BLOCKS = SIDE // J_BLOCK
 STEPS_A_BLOCK = J_BLOCK // J_STEP
 A_FIRST_TURN = 1
 A_HALVES_A_TURN = 2
-PRODUCTS_A_TURN = 4
-PRODUCTS_A_DRAIN_TURN = 6
+PRODUCT_BANKS = 3
+PRODUCTS_A_TURN = 5
 
 FLOPS = 2 * CH * SIDE * SIDE * SIDE
 BYTES = SIDE * SIDE * (CH * (2 + 2 + 4 + 4) + 2 + 2 + 4 + 4) + 2 * CH
@@ -88,12 +88,12 @@ def tile_trianglemultiplicativeupdate_pa_v_kernel(
             nc.vector.memset(ones[:], 1.0)
             w_spread = sums.tile([P, CH], F32, tag="kappa_beta")
             nc.tensor.matmul(out=w_spread[:], lhsT=ones[:], rhs=w_row[:], start=True, stop=True)
+            for engine, codes, scales in ((nc.vector, even_codes, even_scales), (nc.gpsimd, odd_codes, odd_scales)):
+                engine.memset(codes[:], 0)
+                engine.memset(scales[:].rearrange("p d s j -> p (d s j)").bitcast(U32), 0)
             w = once.tile([P, CH], F32)
             nc.vector.tensor_copy(out=w[:], in_=w_spread[:])
             mask_ik_sb = once.tile([P, PACK, SIDE], BF16)
-            for parity in range(2):
-                nc.vector.memset(dx_codes[parity][:], 0)
-                nc.vector.memset(dx_scales[parity][:].rearrange("p d s j -> p (d s j)").bitcast(U32), 0)
 
             loaded = {}
             planes_g = {}
@@ -290,11 +290,14 @@ def tile_trianglemultiplicativeupdate_pa_v_kernel(
                         in_=state[s]["dx"][:, d, :],
                     )
 
-            products = {}
+            filled = []
             woven_tiles = {}
 
-            def multiply_mx(block, kt, lo):
-                product = sums.tile([P, SIDE], F32, bufs=3)
+            def multiply_mx(block, kt, lo, tag):
+                if tag == "product":
+                    product = sums.tile([P, SIDE], F32, tag=tag, bufs=PRODUCT_BANKS)
+                else:
+                    product = sums.tile([P, SIDE], F32, tag=tag)
                 for q in range(HALF_CH):
                     d = lo + q
                     nc.tensor.matmul_mx(
@@ -306,9 +309,11 @@ def tile_trianglemultiplicativeupdate_pa_v_kernel(
                         start=(q == 0),
                         stop=(q == HALF_CH - 1),
                     )
-                products[(block, kt, lo)] = product
+                filled.append((product, block, kt, lo))
 
-            def mask_and_store(block, kt, lo):
+            def mask_and_store():
+                product, block, kt, lo = filled[0]
+                filled.remove(filled[0])
                 if lo == 0:
                     woven = stores.tile([P, J_BLOCK, CH], F32)
                     woven_tiles[(block, kt)] = woven
@@ -316,7 +321,7 @@ def tile_trianglemultiplicativeupdate_pa_v_kernel(
                 cols = slice(block * J_BLOCK, (block + 1) * J_BLOCK)
                 nc.vector.tensor_tensor(
                     out=woven[:, :, lo : lo + HALF_CH],
-                    in0=products[(block, kt, lo)][:].rearrange("p (d j) -> p j d", d=HALF_CH),
+                    in0=product[:].rearrange("p (d j) -> p j d", d=HALF_CH),
                     in1=mask_kj_sb[:, kt, cols].unsqueeze(2).to_broadcast([P, J_BLOCK, HALF_CH]),
                     op=ALU.mult,
                 )
@@ -374,9 +379,8 @@ def tile_trianglemultiplicativeupdate_pa_v_kernel(
             ]
 
             def products_of(turn):
-                most = PRODUCTS_A_TURN if turn < STEPS else PRODUCTS_A_DRAIN_TURN
                 chosen = []
-                while waiting and len(chosen) < most:
+                while waiting and len(chosen) < PRODUCTS_A_TURN:
                     block, kt, lo = waiting[0]
                     dx_turn = (block + 1) * STEPS_A_BLOCK - 1 + 2
                     a_turn = A_FIRST_TURN + (2 * kt + 1) // A_HALVES_A_TURN + 1
@@ -388,91 +392,109 @@ def tile_trianglemultiplicativeupdate_pa_v_kernel(
 
             load(0)
             load(1)
-            nc.sync.dma_start(out=mask_ik_sb[:], in_=mask_ik_rows)
-            load_a(0)
             copy_pairs(0)
             first_rstd = sums.tile([P, 2, COLS], F32, tag="mu_rstd")
             stage_rstd(0, first_rstd)
             lay_out_g(0)
-            for turn in range(STEPS + 2):
+            def empty(count):
+                for i in range(min(count, len(filled))):
+                    mask_and_store()
+
+            for turn in range(STEPS):
                 first, second, third = turn, turn - 1, turn - 2
                 to_fill = products_of(turn)
-                to_empty = list(to_fill)
 
                 def fill(count):
                     for i in range(min(count, len(to_fill))):
                         bank = to_fill[0]
                         to_fill.remove(bank)
-                        multiply_mx(*bank)
-
-                def empty(count):
-                    for i in range(min(count, len(to_empty))):
-                        bank = to_empty[0]
-                        to_empty.remove(bank)
-                        mask_and_store(*bank)
+                        multiply_mx(*bank, "product")
 
                 if turn + 2 < STEPS:
                     load(turn + 2)
+                if turn == 0:
+                    nc.sync.dma_start(out=mask_ik_sb[:], in_=mask_ik_rows)
+                    load_a(0)
                 for half_tile in a_halves_laid_out_in(turn + 1):
                     if half_tile % 2 == 0 and half_tile > 0:
                         load_a(half_tile // 2)
                 if turn == 2:
                     nc.sync.dma_start(out=mask_kj_sb[:], in_=mask_kj_rows)
-                if 0 <= third < STEPS - 1:
+                if 0 <= third:
                     finish_dx(third, nc.gpsimd, slice(0, CH))
                 if first + 1 < STEPS:
                     copy_pairs(first + 1)
                     lay_out_g(first + 1)
-                    if turn > 0:
-                        lay_out_x(first + 1, nc.scalar.copy)
                 fill(1)
-                if third == STEPS - 1:
-                    for lo in range(0, CH, HALF_CH):
-                        finish_dx(third, nc.vector, slice(lo, lo + HALF_CH))
-                        fill(1)
-                        empty(1)
-                        quantise_dx(third, range(lo, lo + HALF_CH))
-                if first < STEPS:
-                    scale_grad(first, (0, 1, 2, 3, 4, 5))
-                if 0 <= second < STEPS:
+                scale_grad(first, (0, 1, 2, 3, 4, 5))
+                if 0 <= second:
                     slope_b(second)
-                if first < STEPS:
-                    scale_grad(first, (6, 7))
-                if 0 <= second < STEPS:
+                scale_grad(first, (6, 7))
+                if 0 <= second:
                     slope_c(second)
-                if first < STEPS:
-                    add_up_hr(first)
+                add_up_hr(first)
                 fill(1)
                 empty(1)
                 for half_tile in a_halves_laid_out_in(turn - 1):
                     mask_a(half_tile // 2, HALF_CH * (half_tile % 2))
                 if turn == 0:
                     lay_out_x(0, nc.vector.tensor_copy)
-                if first < STEPS:
-                    turn_back_mean(first)
-                    stage_pairs(first)
-                    multiply(first, nc.gpsimd if turn > 0 else nc.vector)
-                if turn == 0:
-                    lay_out_x(1, nc.scalar.copy)
-                fill(2)
+                turn_back_mean(first)
+                stage_pairs(first)
+                multiply(first, nc.gpsimd if turn > 0 else nc.vector)
                 for half_tile in a_halves_laid_out_in(turn):
                     lay_out_a(half_tile // 2, HALF_CH * (half_tile % 2))
-                if first < STEPS:
-                    square_rstd(first)
-                if 0 <= second < STEPS:
+                square_rstd(first)
+                if first + 1 < STEPS:
+                    lay_out_x(first + 1, nc.scalar.copy)
+                if 0 <= second:
                     scale_xc(second)
-                    empty(1)
+                fill(2)
+                empty(1)
+                fill(1)
+                if 0 <= second:
                     add_mean(second)
-                if first < STEPS:
-                    correlate(first)
+                empty(1)
+                fill(PRODUCTS_A_TURN)
+                correlate(first)
                 empty(1)
                 for half_tile in a_halves_laid_out_in(turn - 1):
                     quantise_a(half_tile // 2, HALF_CH * (half_tile % 2))
-                if 0 <= third < STEPS - 1:
+                if 0 <= third:
                     quantise_dx(third, range(CH))
-                fill(PRODUCTS_A_DRAIN_TURN)
-                empty(PRODUCTS_A_DRAIN_TURN)
+                empty(PRODUCTS_A_TURN)
 
-            for bank in sorted(waiting, key=lambda bank: (bank[0], bank[2], bank[1])):
-                multiply_mx(*bank)
-                mask_and_store(*bank)
+            bank_cycle = ["keep_ps", "hr_r"] + PRODUCT_BANKS * ["product"] + ["mu_rstd", "mean_prod", "kappa_beta"]
+
+            def fill(count):
+                for i in range(min(count, len(waiting))):
+                    bank = waiting[0]
+                    waiting.remove(bank)
+                    multiply_mx(*bank, bank_cycle[0])
+                    bank_cycle.append(bank_cycle[0])
+                    bank_cycle.remove(bank_cycle[0])
+
+            last = STEPS - 1
+            finish_dx(last - 1, nc.gpsimd, slice(0, CH))
+            fill(1)
+            slope_b(last)
+            slope_c(last)
+            fill(1)
+            empty(1)
+            fill(3)
+            scale_xc(last)
+            empty(1)
+            fill(2)
+            add_mean(last)
+            empty(1)
+            fill(1)
+            quantise_dx(last - 1, range(CH))
+            empty(1)
+            waiting = sorted(waiting, key=lambda bank: (bank[1] // 2, bank[2], bank[1]))
+            for lo in range(0, CH, HALF_CH):
+                finish_dx(last, nc.vector, slice(lo, lo + HALF_CH))
+                empty(1)
+                quantise_dx(last, range(lo, lo + HALF_CH))
+                fill(2)
+            fill(len(waiting))
+            empty(len(filled))

@@ -86,7 +86,7 @@ def tile_trianglemultiplicativeupdate_pa_v_kernel(
             nc.scalar.dma_start(out=w_row[0:1, :], in_=ln_out_w.partition_broadcast(1))
             ones = once.tile([P, P], BF16)
             nc.vector.memset(ones[:], 1.0)
-            w_spread = sums.tile([P, CH], F32, tag="kappa_beta")
+            w_spread = sums.tile([P, CH], F32, tag="mu_mean")
             nc.tensor.matmul(out=w_spread[:], lhsT=ones[:], rhs=w_row[:], start=True, stop=True)
             for engine, codes, scales in ((nc.vector, even_codes, even_scales), (nc.gpsimd, odd_codes, odd_scales)):
                 engine.memset(codes[:], 0)
@@ -94,6 +94,8 @@ def tile_trianglemultiplicativeupdate_pa_v_kernel(
             w = once.tile([P, CH], F32)
             nc.vector.tensor_copy(out=w[:], in_=w_spread[:])
             mask_ik_sb = once.tile([P, PACK, SIDE], BF16)
+            rstd_beta = sums.tile([P, 2, COLS], F32)
+            kappa_prod = sums.tile([P, 2, COLS], F32)
 
             loaded = {}
             planes_g = {}
@@ -142,19 +144,18 @@ def tile_trianglemultiplicativeupdate_pa_v_kernel(
                 nc.scalar.copy(out=m[:].rearrange("p (j t) -> p j t", t=PACK), in_=mu_ld[:].rearrange("p t j -> p j t"))
                 state[s] = {"r": r, "m": m}
 
-            def stage_rstd(s, mu_rstd):
-                nc.tensor.matmul(out=mu_rstd[:, 1, :], lhsT=identity[:], rhs=state[s]["r"][:, 0, :], start=True, stop=True)
-                state[s]["rstd"] = mu_rstd[:, 1, :]
+            def stage_rstd(s):
+                nc.tensor.matmul(out=rstd_beta[:, 0, :], lhsT=identity[:], rhs=state[s]["r"][:, 0, :], start=True, stop=True)
 
             def stage_pairs(s):
-                mu_rstd = sums.tile([P, 2, COLS], F32)
-                if s + 1 < STEPS:
-                    stage_rstd(s + 1, mu_rstd)
+                mu_mean = sums.tile([P, 2, COLS], F32)
                 for b in range(0, COLS, P):
                     nc.tensor.transpose(
-                        out=mu_rstd[:, 0, b : b + P], in_=state[s]["m"][:, b : b + P], identity=identity[:]
+                        out=mu_mean[:, 0, b : b + P], in_=state[s]["m"][:, b : b + P], identity=identity[:]
                     )
-                state[s]["mu_turned"] = mu_rstd[:, 0, :]
+                state[s]["mu_mean"] = mu_mean
+
+            def turn_rstd(s):
                 state[s]["r_turned"] = hr_r_bank(s)[:, 1, :]
                 turn_and_add(state[s]["r"], 1, state[s]["r_turned"])
 
@@ -164,9 +165,15 @@ def tile_trianglemultiplicativeupdate_pa_v_kernel(
                 state[s]["r_sq_turned"] = r_sq_turned
 
             def lay_out_g(s):
-                g = work.tile([P, CH, COLS], BF16)
-                to_planes(g, loaded[s][1], nc.scalar.copy)
-                planes_g[s] = g
+                h = work.tile([P, CH, COLS], F32, bufs=1)
+                for d in range(CH):
+                    h_plane = h[:, d, :].rearrange("p (c t) -> p c t", t=PACK)
+                    g_plane = loaded[s][1][:, :, :, d].rearrange("p t c -> p c t")
+                    if s > 0 or d < HALF_CH:
+                        nc.scalar.activation(out=h_plane, in_=g_plane, func=COPY, scale=w[:, d : d + 1])
+                    else:
+                        nc.vector.tensor_scalar(out=h_plane, in0=g_plane, scalar1=w[:, d : d + 1], scalar2=None, op0=ALU.mult)
+                planes_g[s] = h
 
             def lay_out_x(s, copy):
                 xc = work.tile([P, CH, COLS], F32, bufs=4)
@@ -174,19 +181,16 @@ def tile_trianglemultiplicativeupdate_pa_v_kernel(
                 planes_x[s] = xc
 
             def scale_grad(s, planes):
-                if planes[0] == 0:
-                    hr = work.tile([P, CH, COLS], F32, bufs=3)
-                    state[s]["hr"] = hr
-                hr = state[s]["hr"]
-                for d in planes:
-                    nc.vector.scalar_tensor_tensor(
-                        out=hr[:, d, :],
-                        in0=planes_g[s][:, d, :],
-                        scalar=w[:, d : d + 1],
-                        in1=state[s]["rstd"],
-                        op0=ALU.mult,
-                        op1=ALU.mult,
-                    )
+                nc.vector.tensor_tensor(
+                    out=state[s]["hr"][:, planes, :],
+                    in0=planes_g[s][:, planes, :],
+                    in1=over_planes(rstd_beta[:, 0, :], planes.stop - planes.start),
+                    op=ALU.mult,
+                )
+
+            def open_hr(s):
+                hr = work.tile([P, CH, COLS], F32, bufs=3)
+                state[s]["hr"] = hr
 
             def add_up_hr(s):
                 mean_turned = work.tile([P, COLS], F32)
@@ -195,47 +199,52 @@ def tile_trianglemultiplicativeupdate_pa_v_kernel(
                 state[s]["mean_turned"] = mean_turned
 
             def turn_back_mean(s):
-                mean_prod = sums.tile([P, 2, COLS], F32)
                 for b in range(0, COLS, P):
                     nc.tensor.transpose(
-                        out=mean_prod[:, 0, b : b + P], in_=state[s]["mean_turned"][:, b : b + P], identity=identity[:]
+                        out=state[s]["mu_mean"][:, 1, b : b + P],
+                        in_=state[s]["mean_turned"][:, b : b + P],
+                        identity=identity[:],
                     )
-                state[s]["mean_prod"] = mean_prod
 
             def multiply(s, engine):
                 prod = work.tile([P, CH + 1, COLS], F32, bufs=1)
-                engine.tensor_tensor(out=prod[:, :CH, :], in0=state[s]["hr"][:], in1=planes_x[s][:], op=ALU.mult)
+                width = P if s == 0 else COLS
+                for b in range(0, COLS, width):
+                    engine.tensor_tensor(
+                        out=prod[:, :CH, b : b + width],
+                        in0=state[s]["hr"][:, :, b : b + width],
+                        in1=planes_x[s][:, :, b : b + width],
+                        op=ALU.mult,
+                    )
                 state[s]["prod"] = prod
 
             def correlate(s):
                 prod = state[s]["prod"]
                 nc.vector.scalar_tensor_tensor(
                     out=prod[:, CH, :],
-                    in0=state[s]["mean_prod"][:, 0, :],
+                    in0=state[s]["mu_mean"][:, 1, :],
                     scalar=-1.0 * CH,
                     in1=state[s]["m"][:],
                     op0=ALU.mult,
                     op1=ALU.mult,
                 )
-                turn_and_add(prod, CH + 1, state[s]["mean_prod"][:, 1, :])
+                turn_and_add(prod, CH + 1, kappa_prod[:, 1, :])
 
             def slope_b(s):
                 kappa_turned = work.tile([P, COLS], F32)
                 nc.vector.scalar_tensor_tensor(
                     out=kappa_turned[:],
-                    in0=state[s]["mean_prod"][:, 1, :],
+                    in0=kappa_prod[:, 1, :],
                     scalar=1.0 / CH,
                     in1=state[s]["r_sq_turned"][:],
                     op0=ALU.mult,
                     op1=ALU.mult,
                 )
                 state[s]["kappa_turned"] = kappa_turned
-                kappa_beta = sums.tile([P, 2, COLS], F32)
                 for b in range(0, COLS, P):
                     nc.tensor.transpose(
-                        out=kappa_beta[:, 0, b : b + P], in_=kappa_turned[:, b : b + P], identity=identity[:]
+                        out=kappa_prod[:, 0, b : b + P], in_=kappa_turned[:, b : b + P], identity=identity[:]
                     )
-                state[s]["kappa_beta"] = kappa_beta
 
             def slope_c(s):
                 minus_kappa_mu = work.tile([P, COLS], F32)
@@ -243,14 +252,14 @@ def tile_trianglemultiplicativeupdate_pa_v_kernel(
                     out=minus_kappa_mu[:],
                     in0=state[s]["kappa_turned"][:],
                     scalar=-1.0,
-                    in1=state[s]["mu_turned"],
+                    in1=state[s]["mu_mean"][:, 0, :],
                     op0=ALU.mult,
                     op1=ALU.mult,
                 )
                 for b in range(0, COLS, P):
                     for term, first_term in ((state[s]["mean_turned"], True), (minus_kappa_mu, False)):
                         nc.tensor.matmul(
-                            out=state[s]["kappa_beta"][:, 1, b : b + P],
+                            out=rstd_beta[:, 1, b : b + P],
                             lhsT=term[:, b : b + P],
                             rhs=identity[:],
                             is_transpose=True,
@@ -262,14 +271,14 @@ def tile_trianglemultiplicativeupdate_pa_v_kernel(
                 for lo in range(0, CH, HALF_CH):
                     part = planes_x[s][:, lo : lo + HALF_CH, :]
                     nc.vector.tensor_tensor(
-                        out=part, in0=part, in1=over_planes(state[s]["kappa_beta"][:, 0, :], HALF_CH), op=ALU.mult
+                        out=part, in0=part, in1=over_planes(kappa_prod[:, 0, :], HALF_CH), op=ALU.mult
                     )
 
             def add_mean(s):
                 for lo in range(0, CH, HALF_CH):
                     part = planes_x[s][:, lo : lo + HALF_CH, :]
                     nc.vector.tensor_tensor(
-                        out=part, in0=part, in1=over_planes(state[s]["kappa_beta"][:, 1, :], HALF_CH), op=ALU.add
+                        out=part, in0=part, in1=over_planes(rstd_beta[:, 1, :], HALF_CH), op=ALU.add
                     )
 
             def finish_dx(s, engine, planes):
@@ -348,15 +357,18 @@ def tile_trianglemultiplicativeupdate_pa_v_kernel(
                         out=keep_ik[:].rearrange("p (k t) -> p k t", t=PACK),
                         in_=mask_ik_sb[:, :, kt * K_TILE : (kt + 1) * K_TILE].rearrange("p t k -> p k t"),
                     )
-                    keep_ps = sums.tile([P, K_TILE * PACK], BF16)
-                    nc.tensor.matmul(out=keep_ps[:], lhsT=identity_bf16[:], rhs=keep_ik[:], start=True, stop=True)
-                    keeps[kt] = keep_ps
+                    keeps[kt] = keep_ik
                 a_planes = work.tile([P, HALF_CH, K_TILE * PACK], BF16, align_bytes=64, bufs=4)
                 nc.scalar.copy(
                     out=a_planes[:].rearrange("p d (c t) -> p c t d", t=PACK),
                     in_=a_tiles[kt][:, :, :, lo : lo + HALF_CH].rearrange("p t c d -> p c t d"),
                 )
                 a_halves[(kt, lo)] = a_planes
+
+            def stage_keep(kt):
+                keep_ps = sums.tile([P, K_TILE * PACK], BF16)
+                nc.tensor.matmul(out=keep_ps[:], lhsT=identity_bf16[:], rhs=keeps[kt][:], start=True, stop=True)
+                keeps[kt] = keep_ps
 
             def mask_a(kt, lo):
                 a_planes = a_halves[(kt, lo)]
@@ -393,11 +405,10 @@ def tile_trianglemultiplicativeupdate_pa_v_kernel(
             load(0)
             load(1)
             copy_pairs(0)
-            first_rstd = sums.tile([P, 2, COLS], F32, tag="mu_rstd")
-            stage_rstd(0, first_rstd)
+            stage_rstd(0)
             lay_out_g(0)
-            def empty(count):
-                for i in range(min(count, len(filled))):
+            def empty(count, leave=1):
+                for i in range(min(count, len(filled) - leave)):
                     mask_and_store()
 
             for turn in range(STEPS):
@@ -420,31 +431,46 @@ def tile_trianglemultiplicativeupdate_pa_v_kernel(
                         load_a(half_tile // 2)
                 if turn == 2:
                     nc.sync.dma_start(out=mask_kj_sb[:], in_=mask_kj_rows)
+                open_hr(first)
                 if 0 <= third:
                     finish_dx(third, nc.gpsimd, slice(0, CH))
                 if first + 1 < STEPS:
                     copy_pairs(first + 1)
-                    lay_out_g(first + 1)
+                    if turn > 1:
+                        lay_out_g(first + 1)
                 fill(1)
-                scale_grad(first, (0, 1, 2, 3, 4, 5))
+                if first == 0:
+                    scale_grad(first, slice(HALF_CH, CH))
+                    scale_grad(first, slice(0, HALF_CH))
+                else:
+                    scale_grad(first, slice(0, 6))
                 if 0 <= second:
                     slope_b(second)
-                scale_grad(first, (6, 7))
+                if first > 0:
+                    scale_grad(first, slice(6, CH))
                 if 0 <= second:
                     slope_c(second)
                 add_up_hr(first)
-                fill(1)
+                if turn <= 1:
+                    lay_out_g(first + 1)
+                if turn == 0:
+                    stage_rstd(1)
                 empty(1)
                 for half_tile in a_halves_laid_out_in(turn - 1):
                     mask_a(half_tile // 2, HALF_CH * (half_tile % 2))
                 if turn == 0:
                     lay_out_x(0, nc.vector.tensor_copy)
-                turn_back_mean(first)
                 stage_pairs(first)
+                fill(1)
+                turn_back_mean(first)
+                turn_rstd(first)
                 multiply(first, nc.gpsimd if turn > 0 else nc.vector)
+                if turn <= 1:
+                    square_rstd(first)
                 for half_tile in a_halves_laid_out_in(turn):
                     lay_out_a(half_tile // 2, HALF_CH * (half_tile % 2))
-                square_rstd(first)
+                if turn > 1:
+                    square_rstd(first)
                 if first + 1 < STEPS:
                     lay_out_x(first + 1, nc.scalar.copy)
                 if 0 <= second:
@@ -455,8 +481,13 @@ def tile_trianglemultiplicativeupdate_pa_v_kernel(
                 if 0 <= second:
                     add_mean(second)
                 empty(1)
+                if 0 < turn and first + 1 < STEPS:
+                    stage_rstd(first + 1)
                 fill(PRODUCTS_A_TURN)
                 correlate(first)
+                for half_tile in a_halves_laid_out_in(turn):
+                    if half_tile % 2 == 0:
+                        stage_keep(half_tile // 2)
                 empty(1)
                 for half_tile in a_halves_laid_out_in(turn - 1):
                     quantise_a(half_tile // 2, HALF_CH * (half_tile % 2))
@@ -464,7 +495,7 @@ def tile_trianglemultiplicativeupdate_pa_v_kernel(
                     quantise_dx(third, range(CH))
                 empty(PRODUCTS_A_TURN)
 
-            bank_cycle = ["keep_ps", "hr_r"] + PRODUCT_BANKS * ["product"] + ["mu_rstd", "mean_prod", "kappa_beta"]
+            bank_cycle = ["keep_ps", "hr_r"] + PRODUCT_BANKS * ["product"] + ["mu_mean"]
 
             def fill(count):
                 for i in range(min(count, len(waiting))):
@@ -497,4 +528,4 @@ def tile_trianglemultiplicativeupdate_pa_v_kernel(
                 quantise_dx(last, range(lo, lo + HALF_CH))
                 fill(2)
             fill(len(waiting))
-            empty(len(filled))
+            empty(len(filled), 0)

@@ -88,9 +88,9 @@ def tile_trianglemultiplicativeupdate_pa_v_kernel(
             nc.vector.memset(ones[:], 1.0)
             w_spread = sums.tile([P, CH], F32, tag="mu_mean")
             nc.tensor.matmul(out=w_spread[:], lhsT=ones[:], rhs=w_row[:], start=True, stop=True)
-            for engine, codes, scales in ((nc.vector, even_codes, even_scales), (nc.gpsimd, odd_codes, odd_scales)):
-                engine.memset(codes[:], 0)
-                engine.memset(scales[:].rearrange("p d s j -> p (d s j)").bitcast(U32), 0)
+            for codes, scales in ((even_codes, even_scales), (odd_codes, odd_scales)):
+                nc.vector.memset(codes[:], 0)
+                nc.vector.memset(scales[:].rearrange("p d s j -> p (d s j)").bitcast(U32), 0)
             w = once.tile([P, CH], F32)
             nc.vector.tensor_copy(out=w[:], in_=w_spread[:])
             mask_ik_sb = once.tile([P, PACK, SIDE], BF16)
@@ -165,15 +165,9 @@ def tile_trianglemultiplicativeupdate_pa_v_kernel(
                 state[s]["r_sq_turned"] = r_sq_turned
 
             def lay_out_g(s):
-                h = work.tile([P, CH, COLS], F32, bufs=1)
-                for d in range(CH):
-                    h_plane = h[:, d, :].rearrange("p (c t) -> p c t", t=PACK)
-                    g_plane = loaded[s][1][:, :, :, d].rearrange("p t c -> p c t")
-                    if s > 0 or d < HALF_CH:
-                        nc.scalar.activation(out=h_plane, in_=g_plane, func=COPY, scale=w[:, d : d + 1])
-                    else:
-                        nc.vector.tensor_scalar(out=h_plane, in0=g_plane, scalar1=w[:, d : d + 1], scalar2=None, op0=ALU.mult)
-                planes_g[s] = h
+                g = work.tile([P, CH, COLS], BF16)
+                to_planes(g, loaded[s][1], nc.scalar.copy)
+                planes_g[s] = g
 
             def lay_out_x(s, copy):
                 xc = work.tile([P, CH, COLS], F32, bufs=4)
@@ -181,16 +175,19 @@ def tile_trianglemultiplicativeupdate_pa_v_kernel(
                 planes_x[s] = xc
 
             def scale_grad(s, planes):
-                nc.vector.tensor_tensor(
-                    out=state[s]["hr"][:, planes, :],
-                    in0=planes_g[s][:, planes, :],
-                    in1=over_planes(rstd_beta[:, 0, :], planes.stop - planes.start),
-                    op=ALU.mult,
-                )
-
-            def open_hr(s):
-                hr = work.tile([P, CH, COLS], F32, bufs=3)
-                state[s]["hr"] = hr
+                if planes[0] == 0:
+                    hr = work.tile([P, CH, COLS], F32, bufs=3)
+                    state[s]["hr"] = hr
+                hr = state[s]["hr"]
+                for d in planes:
+                    nc.vector.scalar_tensor_tensor(
+                        out=hr[:, d, :],
+                        in0=planes_g[s][:, d, :],
+                        scalar=w[:, d : d + 1],
+                        in1=rstd_beta[:, 0, :],
+                        op0=ALU.mult,
+                        op1=ALU.mult,
+                    )
 
             def add_up_hr(s):
                 mean_turned = work.tile([P, COLS], F32)
@@ -431,7 +428,6 @@ def tile_trianglemultiplicativeupdate_pa_v_kernel(
                         load_a(half_tile // 2)
                 if turn == 2:
                     nc.sync.dma_start(out=mask_kj_sb[:], in_=mask_kj_rows)
-                open_hr(first)
                 if 0 <= third:
                     finish_dx(third, nc.gpsimd, slice(0, CH))
                 if first + 1 < STEPS:
@@ -439,15 +435,10 @@ def tile_trianglemultiplicativeupdate_pa_v_kernel(
                     if turn > 1:
                         lay_out_g(first + 1)
                 fill(1)
-                if first == 0:
-                    scale_grad(first, slice(HALF_CH, CH))
-                    scale_grad(first, slice(0, HALF_CH))
-                else:
-                    scale_grad(first, slice(0, 6))
+                scale_grad(first, (0, 1, 2, 3, 4, 5))
                 if 0 <= second:
                     slope_b(second)
-                if first > 0:
-                    scale_grad(first, slice(6, CH))
+                scale_grad(first, (6, 7))
                 if 0 <= second:
                     slope_c(second)
                 add_up_hr(first)

@@ -25,6 +25,7 @@ K_TILES = SIDE // K_TILE
 J_BLOCK = SIDE // HALF_CH
 BLOCKS = SIDE // J_BLOCK
 STEPS_A_BLOCK = J_BLOCK // J_STEP
+PARTS = 2 * 5 + 2 * 5 + 1
 A_FIRST_TURN = 1
 A_HALVES_A_TURN = 2
 PRODUCT_BANKS = 3
@@ -37,6 +38,13 @@ BYTES = SIDE * SIDE * (CH * (2 + 2 + 4 + 4) + 2 + 2 + 4 + 4) + 2 * CH
 def a_halves_laid_out_in(turn):
     first_half = A_HALVES_A_TURN * (turn - A_FIRST_TURN)
     return [half for half in range(first_half, first_half + A_HALVES_A_TURN) if 0 <= half < 2 * K_TILES]
+
+
+def window_of(d):
+    half, slot = divmod(d, HALF_CH)
+    if slot in (0, HALF_CH - 1):
+        return 5 * half + (1 if slot > 0 else 0)
+    return 10 + 5 * half + 2 * (slot - 1)
 
 
 def tile_trianglemultiplicativeupdate_pa_v_kernel(
@@ -66,17 +74,17 @@ def tile_trianglemultiplicativeupdate_pa_v_kernel(
     with tc.manual_schedule(), tc.tile_pool(name="keep", bufs=1) as keep:
         a_codes = keep.tile([P, K_TILES, CH, K_TILE], U32, align_bytes=64)
         a_scales = keep.tile([P, K_TILES, CH, K_TILE], U8, align_bytes=64)
-        even_codes = keep.tile([P, CH, HALF_CH, J_BLOCK], U32, align_bytes=64)
-        even_scales = keep.tile([P, CH, HALF_CH, J_BLOCK], U8, align_bytes=64)
-        odd_codes = keep.tile([P, CH, HALF_CH, J_BLOCK], U32, align_bytes=64)
-        odd_scales = keep.tile([P, CH, HALF_CH, J_BLOCK], U8, align_bytes=64)
+        even_codes = keep.tile([P, PARTS, J_BLOCK], U32, align_bytes=64)
+        even_scales = keep.tile([P, PARTS, J_BLOCK], U8, align_bytes=64)
+        odd_codes = keep.tile([P, PARTS, J_BLOCK], U32, align_bytes=64)
+        odd_scales = keep.tile([P, PARTS, J_BLOCK], U8, align_bytes=64)
         dx_codes = (even_codes, odd_codes)
         dx_scales = (even_scales, odd_scales)
         mask_kj_sb = keep.tile([P, K_TILES, SIDE], BF16)
 
         with tc.tile_pool(name="once", bufs=1) as once, tc.tile_pool(name="loads", bufs=2) as loads, tc.tile_pool(
             name="work", bufs=2
-        ) as work, tc.tile_pool(name="stores", bufs=4) as stores, tc.psum_pool(name="sums", bufs=1) as sums:
+        ) as work, tc.tile_pool(name="stores", bufs=6) as stores, tc.psum_pool(name="sums", bufs=1) as sums:
             identity = once.tile([P, P], F32)
             make_identity(nc, identity[:])
             identity_bf16 = once.tile([P, P], BF16)
@@ -90,7 +98,7 @@ def tile_trianglemultiplicativeupdate_pa_v_kernel(
             nc.tensor.matmul(out=w_spread[:], lhsT=ones[:], rhs=w_row[:], start=True, stop=True)
             for codes, scales in ((even_codes, even_scales), (odd_codes, odd_scales)):
                 nc.vector.memset(codes[:], 0)
-                nc.vector.memset(scales[:].rearrange("p d s j -> p (d s j)").bitcast(U32), 0)
+                nc.vector.memset(scales[:].rearrange("p b j -> p (b j)").bitcast(U32), 0)
             w = once.tile([P, CH], F32)
             nc.vector.tensor_copy(out=w[:], in_=w_spread[:])
             mask_ik_sb = once.tile([P, PACK, SIDE], BF16)
@@ -106,10 +114,10 @@ def tile_trianglemultiplicativeupdate_pa_v_kernel(
                 cols = slice(s * J_STEP, (s + 1) * J_STEP)
                 rstd_ld = loads.tile([P, PACK, J_STEP], F32)
                 nc.sync.dma_start(out=rstd_ld[:], in_=rstd_rows[:, :, cols])
-                mu_ld = loads.tile([P, PACK, J_STEP], F32)
-                nc.sync.dma_start(out=mu_ld[:], in_=mu_rows[:, :, cols])
                 g_ld = loads.tile([P, PACK, J_STEP, CH], BF16)
                 nc.sync.dma_start(out=g_ld[:], in_=g_rows[:, :, cols, :])
+                mu_ld = loads.tile([P, PACK, J_STEP], F32)
+                nc.sync.dma_start(out=mu_ld[:], in_=mu_rows[:, :, cols])
                 x_ld = loads.tile([P, PACK, J_STEP, CH], F32)
                 nc.sync.dma_start(out=x_ld[:], in_=x_rows[:, :, cols, :])
                 loaded[s] = (rstd_ld, g_ld, mu_ld, x_ld)
@@ -134,15 +142,19 @@ def tile_trianglemultiplicativeupdate_pa_v_kernel(
                     hr_r_banks[turn_no] = hr_r
                 return hr_r_banks[turn_no]
 
-            def copy_pairs(s):
-                rstd_ld, g_ld, mu_ld, x_ld = loaded[s]
+            def copy_rstd(s):
                 r = work.tile([P, 1, COLS], F32)
                 nc.scalar.copy(
-                    out=r[:, 0, :].rearrange("p (j t) -> p j t", t=PACK), in_=rstd_ld[:].rearrange("p t j -> p j t")
+                    out=r[:, 0, :].rearrange("p (j t) -> p j t", t=PACK), in_=loaded[s][0][:].rearrange("p t j -> p j t")
                 )
+                state[s] = {"r": r}
+
+            def copy_mu(s):
                 m = work.tile([P, COLS], F32)
-                nc.scalar.copy(out=m[:].rearrange("p (j t) -> p j t", t=PACK), in_=mu_ld[:].rearrange("p t j -> p j t"))
-                state[s] = {"r": r, "m": m}
+                nc.scalar.copy(
+                    out=m[:].rearrange("p (j t) -> p j t", t=PACK), in_=loaded[s][2][:].rearrange("p t j -> p j t")
+                )
+                state[s]["m"] = m
 
             def stage_rstd(s):
                 nc.tensor.matmul(out=rstd_beta[:, 0, :], lhsT=identity[:], rhs=state[s]["r"][:, 0, :], start=True, stop=True)
@@ -290,9 +302,10 @@ def tile_trianglemultiplicativeupdate_pa_v_kernel(
                 block, part = divmod(s, STEPS_A_BLOCK)
                 cols = slice(part * J_STEP, (part + 1) * J_STEP)
                 for d in planes:
+                    own = window_of(d) + d % HALF_CH
                     nc.vector.quantize_mx(
-                        out=dx_codes[block % 2][:, d, d % HALF_CH, cols].bitcast(E5M2_X4),
-                        scales=dx_scales[block % 2][:, d, d % HALF_CH, cols],
+                        out=dx_codes[block % 2][:, own, cols].bitcast(E5M2_X4),
+                        scales=dx_scales[block % 2][:, own, cols],
                         in_=state[s]["dx"][:, d, :],
                     )
 
@@ -306,12 +319,13 @@ def tile_trianglemultiplicativeupdate_pa_v_kernel(
                     product = sums.tile([P, SIDE], F32, tag=tag)
                 for q in range(HALF_CH):
                     d = lo + q
+                    window = slice(window_of(d), window_of(d) + HALF_CH)
                     nc.tensor.matmul_mx(
                         out=product[:],
                         lhsT=a_codes[:, kt, d, :].bitcast(E4M3_X4),
                         lhsT_scale=a_scales[:, kt, d, :],
-                        rhs=dx_codes[block % 2][:, d, :, :].rearrange("p s j -> p (s j)").bitcast(E5M2_X4),
-                        rhs_scale=dx_scales[block % 2][:, d, :, :].rearrange("p s j -> p (s j)"),
+                        rhs=dx_codes[block % 2][:, window, :].rearrange("p b j -> p (b j)").bitcast(E5M2_X4),
+                        rhs_scale=dx_scales[block % 2][:, window, :].rearrange("p b j -> p (b j)"),
                         start=(q == 0),
                         stop=(q == HALF_CH - 1),
                     )
@@ -324,18 +338,21 @@ def tile_trianglemultiplicativeupdate_pa_v_kernel(
                     woven = stores.tile([P, J_BLOCK, CH], F32)
                     woven_tiles[(block, kt)] = woven
                 woven = woven_tiles[(block, kt)]
-                cols = slice(block * J_BLOCK, (block + 1) * J_BLOCK)
-                nc.vector.tensor_tensor(
-                    out=woven[:, :, lo : lo + HALF_CH],
-                    in0=product[:].rearrange("p (d j) -> p j d", d=HALF_CH),
-                    in1=mask_kj_sb[:, kt, cols].unsqueeze(2).to_broadcast([P, J_BLOCK, HALF_CH]),
-                    op=ALU.mult,
-                )
-                if lo > 0:
-                    nc.sync.dma_start(
-                        out=out_rows[kt][:, block * J_BLOCK * CH : (block + 1) * J_BLOCK * CH],
-                        in_=woven[:].rearrange("p j d -> p (j d)"),
+                pieces = 2 if (block, kt) == (BLOCKS - 1, K_TILES - 1) and lo > 0 else 1
+                width = J_BLOCK // pieces
+                for j in range(0, J_BLOCK, width):
+                    first_j = block * J_BLOCK + j
+                    nc.vector.tensor_tensor(
+                        out=woven[:, j : j + width, lo : lo + HALF_CH],
+                        in0=product[:].rearrange("p (d j) -> p j d", d=HALF_CH)[:, j : j + width, :],
+                        in1=mask_kj_sb[:, kt, first_j : first_j + width].unsqueeze(2).to_broadcast([P, width, HALF_CH]),
+                        op=ALU.mult,
                     )
+                    if lo > 0:
+                        nc.sync.dma_start(
+                            out=out_rows[kt][:, first_j * CH : (first_j + width) * CH],
+                            in_=woven[:, j : j + width, :].rearrange("p j d -> p (j d)"),
+                        )
 
             a_tiles = {}
 
@@ -401,9 +418,10 @@ def tile_trianglemultiplicativeupdate_pa_v_kernel(
 
             load(0)
             load(1)
-            copy_pairs(0)
+            copy_rstd(0)
             stage_rstd(0)
             lay_out_g(0)
+            copy_mu(0)
             def empty(count, leave=1):
                 for i in range(min(count, len(filled) - leave)):
                     mask_and_store()
@@ -431,7 +449,8 @@ def tile_trianglemultiplicativeupdate_pa_v_kernel(
                 if 0 <= third:
                     finish_dx(third, nc.gpsimd, slice(0, CH))
                 if first + 1 < STEPS:
-                    copy_pairs(first + 1)
+                    copy_rstd(first + 1)
+                    copy_mu(first + 1)
                     if turn > 1:
                         lay_out_g(first + 1)
                 fill(1)

@@ -27,7 +27,6 @@ BLOCKS = SIDE // J_BLOCK
 STEPS_A_BLOCK = J_BLOCK // J_STEP
 PARTS = 2 * 5 + 2 * 5 + 1
 A_FIRST_TURN = 1
-A_HALVES_A_TURN = 2
 PRODUCT_BANKS = 3
 PRODUCTS_A_TURN = 5
 
@@ -35,9 +34,8 @@ FLOPS = 2 * CH * SIDE * SIDE * SIDE
 BYTES = SIDE * SIDE * (CH * (2 + 2 + 4 + 4) + 2 + 2 + 4 + 4) + 2 * CH
 
 
-def a_halves_laid_out_in(turn):
-    first_half = A_HALVES_A_TURN * (turn - A_FIRST_TURN)
-    return [half for half in range(first_half, first_half + A_HALVES_A_TURN) if 0 <= half < 2 * K_TILES]
+def a_tiles_laid_out_in(turn):
+    return [turn - A_FIRST_TURN] if 0 <= turn - A_FIRST_TURN < K_TILES else []
 
 
 def window_of(d):
@@ -177,8 +175,11 @@ def tile_trianglemultiplicativeupdate_pa_v_kernel(
                 state[s]["r_sq_turned"] = r_sq_turned
 
             def lay_out_g(s):
-                g = work.tile([P, CH, COLS], BF16)
-                to_planes(g, loaded[s][1], nc.scalar.copy)
+                g = work.tile([P, CH // 2, COLS, 2], BF16)
+                nc.scalar.copy(
+                    out=g[:].rearrange("p w c i -> p w (c i)").bitcast(U32).rearrange("p w (c t) -> p c t w", t=PACK),
+                    in_=loaded[s][1][:].rearrange("p t c d -> p t (c d)").bitcast(U32).rearrange("p t (c w) -> p c t w", w=CH // 2),
+                )
                 planes_g[s] = g
 
             def lay_out_x(s, copy):
@@ -194,7 +195,7 @@ def tile_trianglemultiplicativeupdate_pa_v_kernel(
                 for d in planes:
                     nc.vector.scalar_tensor_tensor(
                         out=hr[:, d, :],
-                        in0=planes_g[s][:, d, :],
+                        in0=planes_g[s][:, d // 2, :, d % 2],
                         scalar=w[:, d : d + 1],
                         in1=rstd_beta[:, 0, :],
                         op0=ALU.mult,
@@ -361,7 +362,7 @@ def tile_trianglemultiplicativeupdate_pa_v_kernel(
                 nc.sync.dma_start(out=a_ld[:], in_=a_rows[:, :, kt * K_TILE : (kt + 1) * K_TILE, :])
                 a_tiles[kt] = a_ld
 
-            a_halves = {}
+            planes_a = {}
             keeps = {}
 
             def lay_out_a(kt, lo):
@@ -372,32 +373,32 @@ def tile_trianglemultiplicativeupdate_pa_v_kernel(
                         in_=mask_ik_sb[:, :, kt * K_TILE : (kt + 1) * K_TILE].rearrange("p t k -> p k t"),
                     )
                     keeps[kt] = keep_ik
-                a_planes = work.tile([P, HALF_CH, K_TILE * PACK], BF16, align_bytes=64, bufs=4)
+                    a_planes = work.tile([P, CH, K_TILE * PACK], BF16, align_bytes=64)
+                    planes_a[kt] = a_planes
                 nc.scalar.copy(
-                    out=a_planes[:].rearrange("p d (c t) -> p c t d", t=PACK),
+                    out=planes_a[kt][:, lo : lo + HALF_CH, :].rearrange("p d (c t) -> p c t d", t=PACK),
                     in_=a_tiles[kt][:, :, :, lo : lo + HALF_CH].rearrange("p t c d -> p c t d"),
                 )
-                a_halves[(kt, lo)] = a_planes
 
             def stage_keep(kt):
                 keep_ps = sums.tile([P, K_TILE * PACK], BF16)
                 nc.tensor.matmul(out=keep_ps[:], lhsT=identity_bf16[:], rhs=keeps[kt][:], start=True, stop=True)
                 keeps[kt] = keep_ps
 
-            def mask_a(kt, lo):
-                a_planes = a_halves[(kt, lo)]
+            def mask_a(kt):
+                a_planes = planes_a[kt]
                 nc.vector.tensor_tensor(
                     out=a_planes[:],
                     in0=a_planes[:],
-                    in1=keeps[kt][:].unsqueeze(1).to_broadcast([P, HALF_CH, K_TILE * PACK]),
+                    in1=keeps[kt][:].unsqueeze(1).to_broadcast([P, CH, K_TILE * PACK]),
                     op=ALU.mult,
                 )
 
-            def quantise_a(kt, lo):
+            def quantise_a(kt):
                 nc.vector.quantize_mx(
-                    out=a_codes[:, kt, lo : lo + HALF_CH, :].rearrange("p d k -> p (d k)").bitcast(E4M3_X4),
-                    scales=a_scales[:, kt, lo : lo + HALF_CH, :].rearrange("p d k -> p (d k)"),
-                    in_=a_halves[(kt, lo)][:].rearrange("p d c -> p (d c)"),
+                    out=a_codes[:, kt, :, :].rearrange("p d k -> p (d k)").bitcast(E4M3_X4),
+                    scales=a_scales[:, kt, :, :].rearrange("p d k -> p (d k)"),
+                    in_=planes_a[kt][:].rearrange("p d c -> p (d c)"),
                 )
 
             waiting = [
@@ -409,7 +410,7 @@ def tile_trianglemultiplicativeupdate_pa_v_kernel(
                 while waiting and len(chosen) < PRODUCTS_A_TURN:
                     block, kt, lo = waiting[0]
                     dx_turn = (block + 1) * STEPS_A_BLOCK - 1 + 2
-                    a_turn = A_FIRST_TURN + (2 * kt + 1) // A_HALVES_A_TURN + 1
+                    a_turn = A_FIRST_TURN + kt + 1
                     if max(dx_turn, a_turn) >= turn:
                         break
                     chosen.append(waiting[0])
@@ -436,18 +437,20 @@ def tile_trianglemultiplicativeupdate_pa_v_kernel(
                         to_fill.remove(bank)
                         multiply_mx(*bank, "product")
 
-                if turn + 2 < STEPS:
-                    load(turn + 2)
                 if turn == 0:
                     nc.sync.dma_start(out=mask_ik_sb[:], in_=mask_ik_rows)
                     load_a(0)
-                for half_tile in a_halves_laid_out_in(turn + 1):
-                    if half_tile % 2 == 0 and half_tile > 0:
-                        load_a(half_tile // 2)
+                if turn + 2 < STEPS:
+                    load(turn + 2)
+                for kt in a_tiles_laid_out_in(turn + 1):
+                    if kt > 0:
+                        load_a(kt)
                 if turn == 2:
                     nc.sync.dma_start(out=mask_kj_sb[:], in_=mask_kj_rows)
                 if 0 <= third:
                     finish_dx(third, nc.gpsimd, slice(0, CH))
+                if turn == 1:
+                    lay_out_a(0, 0)
                 if first + 1 < STEPS:
                     copy_rstd(first + 1)
                     copy_mu(first + 1)
@@ -466,8 +469,8 @@ def tile_trianglemultiplicativeupdate_pa_v_kernel(
                 if turn == 0:
                     stage_rstd(1)
                 empty(1)
-                for half_tile in a_halves_laid_out_in(turn - 1):
-                    mask_a(half_tile // 2, HALF_CH * (half_tile % 2))
+                for kt in a_tiles_laid_out_in(turn - 1):
+                    mask_a(kt)
                 if turn == 0:
                     lay_out_x(0, nc.vector.tensor_copy)
                 stage_pairs(first)
@@ -477,8 +480,10 @@ def tile_trianglemultiplicativeupdate_pa_v_kernel(
                 multiply(first, nc.gpsimd if turn > 0 else nc.vector)
                 if turn <= 1:
                     square_rstd(first)
-                for half_tile in a_halves_laid_out_in(turn):
-                    lay_out_a(half_tile // 2, HALF_CH * (half_tile % 2))
+                for kt in a_tiles_laid_out_in(turn):
+                    if turn > 1:
+                        lay_out_a(kt, 0)
+                    lay_out_a(kt, HALF_CH)
                 if turn > 1:
                     square_rstd(first)
                 if first + 1 < STEPS:
@@ -495,12 +500,11 @@ def tile_trianglemultiplicativeupdate_pa_v_kernel(
                     stage_rstd(first + 1)
                 fill(PRODUCTS_A_TURN)
                 correlate(first)
-                for half_tile in a_halves_laid_out_in(turn):
-                    if half_tile % 2 == 0:
-                        stage_keep(half_tile // 2)
+                for kt in a_tiles_laid_out_in(turn):
+                    stage_keep(kt)
                 empty(1)
-                for half_tile in a_halves_laid_out_in(turn - 1):
-                    quantise_a(half_tile // 2, HALF_CH * (half_tile % 2))
+                for kt in a_tiles_laid_out_in(turn - 1):
+                    quantise_a(kt)
                 if 0 <= third:
                     quantise_dx(third, range(CH))
                 empty(PRODUCTS_A_TURN)

@@ -28,7 +28,7 @@ STEPS_A_BLOCK = J_BLOCK // J_STEP
 PARTS = 2 * 5 + 2 * 5 + 1
 A_FIRST_TURN = 1
 PRODUCT_BANKS = 3
-PRODUCTS_A_TURN = 5
+PRODUCTS_A_TURN = 6
 
 FLOPS = 2 * CH * SIDE * SIDE * SIDE
 BYTES = SIDE * SIDE * (CH * (2 + 2 + 4 + 4) + 2 + 2 + 4 + 4) + 2 * CH
@@ -92,13 +92,15 @@ def tile_trianglemultiplicativeupdate_pa_v_kernel(
             nc.scalar.dma_start(out=w_row[0:1, :], in_=ln_out_w.partition_broadcast(1))
             ones = once.tile([P, P], BF16)
             nc.vector.memset(ones[:], 1.0)
-            w_spread = sums.tile([P, CH], F32, tag="mu_mean")
-            nc.tensor.matmul(out=w_spread[:], lhsT=ones[:], rhs=w_row[:], start=True, stop=True)
             for codes, scales in ((even_codes, even_scales), (odd_codes, odd_scales)):
-                nc.vector.memset(codes[:], 0)
-                nc.vector.memset(scales[:].rearrange("p b j -> p (b j)").bitcast(U32), 0)
+                words = scales[:].rearrange("p b j -> p (b j)").bitcast(U32).rearrange("p (b j) -> p b j", b=PARTS)
+                for parts in (codes, words):
+                    rows = parts[:, : PARTS - 1, :].rearrange("p (r c) j -> p r c j", c=5)
+                    nc.vector.memset(rows[:, :, 2:4, :], 0)
+                    nc.vector.memset(rows[:, 0:2, 1, :], 0)
+                    nc.vector.memset(rows[:, 2:4, 0, :], 0)
+                    nc.vector.memset(parts[:, PARTS - 1, :], 0)
             w = once.tile([P, CH], F32)
-            nc.vector.tensor_copy(out=w[:], in_=w_spread[:])
             mask_ik_sb = once.tile([P, PACK, SIDE], BF16)
             rstd_beta = sums.tile([P, 2, COLS], F32)
             kappa_prod = sums.tile([P, 2, COLS], F32)
@@ -176,10 +178,15 @@ def tile_trianglemultiplicativeupdate_pa_v_kernel(
 
             def lay_out_g(s):
                 g = work.tile([P, CH // 2, COLS, 2], BF16)
-                nc.scalar.copy(
-                    out=g[:].rearrange("p w c i -> p w (c i)").bitcast(U32).rearrange("p w (c t) -> p c t w", t=PACK),
-                    in_=loaded[s][1][:].rearrange("p t c d -> p t (c d)").bitcast(U32).rearrange("p t (c w) -> p c t w", w=CH // 2),
-                )
+                count = CH // 4 if s == 0 else CH // 2
+                for lo in range(0, CH // 2, count):
+                    nc.scalar.copy(
+                        out=g[:, lo : lo + count].rearrange("p w c i -> p w (c i)").bitcast(U32).rearrange("p w (c t) -> p c t w", t=PACK),
+                        in_=loaded[s][1][:]
+                        .rearrange("p t c d -> p t (c d)")
+                        .bitcast(U32)
+                        .rearrange("p t (c w) -> p c t w", w=CH // 2)[:, :, :, lo : lo + count],
+                    )
                 planes_g[s] = g
 
             def lay_out_x(s, copy):
@@ -421,6 +428,9 @@ def tile_trianglemultiplicativeupdate_pa_v_kernel(
             load(1)
             copy_rstd(0)
             stage_rstd(0)
+            w_spread = sums.tile([P, CH], F32, tag="mu_mean")
+            nc.tensor.matmul(out=w_spread[:], lhsT=ones[:], rhs=w_row[:], start=True, stop=True)
+            nc.vector.tensor_copy(out=w[:], in_=w_spread[:])
             lay_out_g(0)
             copy_mu(0)
             def empty(count, leave=1):

import concourse.mybir as mybir
from concourse.masks import make_identity

F32 = mybir.dt.float32
BF16 = mybir.dt.bfloat16
U32 = mybir.dt.uint32
U8 = mybir.dt.uint8
E4M3_X4 = mybir.dt.float8_e4m3fn_x4
E5M2_X4 = mybir.dt.float8_e5m2_x4
ALU = mybir.AluOpType
SQUARE = mybir.ActivationFunctionType.Square
COPY = mybir.ActivationFunctionType.Copy

P = 128
PACK = 4
SIDE = 512
HALF_SIDE = SIDE // 2
CH = 8
HALF_CH = 4
J_STEP = 64
STEPS = SIDE // J_STEP
COLS = J_STEP * PACK
K_TILE = 128
K_TILES = SIDE // K_TILE
J_BLOCK = SIDE // HALF_CH
BLOCKS = SIDE // J_BLOCK
STEPS_A_BLOCK = J_BLOCK // J_STEP
PARTS = 2 * 5 + 2 * 5 + 1
A_FIRST_TURN = 1
PRODUCT_BANKS = 3
PRODUCTS_A_TURN = 6

FLOPS = 2 * CH * SIDE * SIDE * SIDE
BYTES = SIDE * SIDE * (CH * (2 + 2 + 4 + 4) + 2 + 2 + 4 + 4) + 2 * CH


def a_tiles_laid_out_in(turn):
    return [turn - A_FIRST_TURN] if 0 <= turn - A_FIRST_TURN < K_TILES else []


def window_of(d):
    half, slot = divmod(d, HALF_CH)
    if slot in (0, HALF_CH - 1):
        return 5 * half + (1 if slot > 0 else 0)
    return 10 + 5 * half + 2 * (slot - 1)


def tile_trianglemultiplicativeupdate_pa_v_kernel(
    tc, a_gated, b_gated, mask_ik, mask_kj, ln_out_w, ln_out_b, x, mu, rstd, grad_out, out
):
    nc = tc.nc

    a_rows = a_gated[0].rearrange("(p t) k d -> p t k d", t=PACK)
    mask_ik_rows = mask_ik[0].rearrange("(p t) k -> p t k", t=PACK)
    x_rows = x[0].rearrange("(p t) j d -> p t j d", t=PACK)
    g_rows = grad_out[0].rearrange("(p t) j d -> p t j d", t=PACK)
    mu_rows = mu[0].rearrange("(p t) j -> p t j", t=PACK)
    rstd_rows = rstd[0].rearrange("(p t) j -> p t j", t=PACK)
    mask_kj_rows = mask_kj[0].rearrange("(kt p) j -> p kt j", p=P)
    out_rows = out[0].rearrange("(kt p) j d -> kt p (j d)", p=P)

    def to_planes(planes, loaded, copy):
        for d in range(0, CH, HALF_CH):
            copy(
                out=planes[:, d : d + HALF_CH, :].rearrange("p d (c t) -> p c t d", t=PACK),
                in_=loaded[:, :, :, d : d + HALF_CH].rearrange("p t c d -> p c t d"),
            )

    def over_planes(per_pair, count):
        return per_pair.unsqueeze(1).to_broadcast([P, count, COLS])

    with tc.manual_schedule(), tc.tile_pool(name="keep", bufs=1) as keep:
        a_codes = keep.tile([P, K_TILES, CH, K_TILE], U32, align_bytes=64)
        a_scales = keep.tile([P, K_TILES, CH, K_TILE], U8, align_bytes=64)
        even_codes = keep.tile([P, PARTS, J_BLOCK], U32, align_bytes=64)
        even_scales = keep.tile([P, PARTS, J_BLOCK], U8, align_bytes=64)
        odd_codes = keep.tile([P, PARTS, J_BLOCK], U32, align_bytes=64)
        odd_scales = keep.tile([P, PARTS, J_BLOCK], U8, align_bytes=64)
        dx_codes = (even_codes, odd_codes)
        dx_scales = (even_scales, odd_scales)
        mask_kj_sb = keep.tile([P, K_TILES, SIDE], BF16)

        with tc.tile_pool(name="once", bufs=1) as once, tc.tile_pool(name="loads", bufs=2) as loads, tc.tile_pool(
            name="work", bufs=2
        ) as work, tc.tile_pool(name="stores", bufs=6) as stores, tc.psum_pool(name="sums", bufs=1) as sums:
            identity = once.tile([P, P], F32)
            make_identity(nc, identity[:])
            identity_bf16 = once.tile([P, P], BF16)
            make_identity(nc, identity_bf16[:])
            w_row = once.tile([P, CH], BF16)
            nc.vector.memset(w_row[:], 0.0)
            nc.scalar.dma_start(out=w_row[0:1, :], in_=ln_out_w.partition_broadcast(1))
            ones = once.tile([P, P], BF16)
            nc.vector.memset(ones[:], 1.0)
            for codes, scales in ((even_codes, even_scales), (odd_codes, odd_scales)):
                words = scales[:].rearrange("p b j -> p (b j)").bitcast(U32).rearrange("p (b j) -> p b j", b=PARTS)
                for parts in (codes, words):
                    rows = parts[:, : PARTS - 1, :].rearrange("p (r c) j -> p r c j", c=5)
                    nc.vector.memset(rows[:, :, 2:4, :], 0)
                    nc.vector.memset(rows[:, 0:2, 1, :], 0)
                    nc.vector.memset(rows[:, 2:4, 0, :], 0)
                    nc.vector.memset(parts[:, PARTS - 1, :], 0)
            w = once.tile([P, CH], F32)
            mask_ik_sb = once.tile([P, PACK, SIDE], BF16)
            rstd_beta = sums.tile([P, 2, COLS], F32)
            kappa_prod = sums.tile([P, 2, COLS], F32)

            loaded = {}
            planes_g = {}
            planes_x = {}
            state = {}

            def load(s):
                cols = slice(s * J_STEP, (s + 1) * J_STEP)
                rstd_ld = loads.tile([P, PACK, J_STEP], F32)
                nc.sync.dma_start(out=rstd_ld[:], in_=rstd_rows[:, :, cols])
                g_ld = loads.tile([P, PACK, J_STEP, CH], BF16)
                nc.sync.dma_start(out=g_ld[:], in_=g_rows[:, :, cols, :])
                mu_ld = loads.tile([P, PACK, J_STEP], F32)
                nc.sync.dma_start(out=mu_ld[:], in_=mu_rows[:, :, cols])
                x_ld = loads.tile([P, PACK, J_STEP, CH], F32)
                nc.sync.dma_start(out=x_ld[:], in_=x_rows[:, :, cols, :])
                loaded[s] = (rstd_ld, g_ld, mu_ld, x_ld)

            def turn_and_add(planes, count, turned):
                for b in range(0, COLS, P):
                    for d in range(count):
                        nc.tensor.matmul(
                            out=turned[:, b : b + P],
                            lhsT=planes[:, d, b : b + P],
                            rhs=identity[:],
                            is_transpose=True,
                            start=(d == 0),
                            stop=(d == count - 1),
                        )

            hr_r_banks = {}

            def hr_r_bank(turn_no):
                if turn_no not in hr_r_banks:
                    hr_r = sums.tile([P, 2, COLS], F32)
                    hr_r_banks[turn_no] = hr_r
                return hr_r_banks[turn_no]

            def copy_rstd(s):
                r = work.tile([P, 1, COLS], F32)
                nc.scalar.copy(
                    out=r[:, 0, :].rearrange("p (j t) -> p j t", t=PACK), in_=loaded[s][0][:].rearrange("p t j -> p j t")
                )
                state[s] = {"r": r}

            def copy_mu(s):
                m = work.tile([P, COLS], F32)
                nc.scalar.copy(
                    out=m[:].rearrange("p (j t) -> p j t", t=PACK), in_=loaded[s][2][:].rearrange("p t j -> p j t")
                )
                state[s]["m"] = m

            def stage_rstd(s):
                nc.tensor.matmul(out=rstd_beta[:, 0, :], lhsT=identity[:], rhs=state[s]["r"][:, 0, :], start=True, stop=True)

            def stage_pairs(s):
                mu_mean = sums.tile([P, 2, COLS], F32)
                for b in range(0, COLS, P):
                    nc.tensor.transpose(
                        out=mu_mean[:, 0, b : b + P], in_=state[s]["m"][:, b : b + P], identity=identity[:]
                    )
                state[s]["mu_mean"] = mu_mean

            def turn_rstd(s):
                state[s]["r_turned"] = hr_r_bank(s)[:, 1, :]
                turn_and_add(state[s]["r"], 1, state[s]["r_turned"])

            def square_rstd(s):
                r_sq_turned = work.tile([P, COLS], F32)
                nc.scalar.activation(out=r_sq_turned[:], in_=state[s]["r_turned"], func=SQUARE)
                state[s]["r_sq_turned"] = r_sq_turned

            def lay_out_g(s):
                g = work.tile([P, CH // 2, COLS, 2], BF16)
                count = CH // 4 if s == 0 else CH // 2
                for lo in range(0, CH // 2, count):
                    nc.scalar.copy(
                        out=g[:, lo : lo + count].rearrange("p w c i -> p w (c i)").bitcast(U32).rearrange("p w (c t) -> p c t w", t=PACK),
                        in_=loaded[s][1][:]
                        .rearrange("p t c d -> p t (c d)")
                        .bitcast(U32)
                        .rearrange("p t (c w) -> p c t w", w=CH // 2)[:, :, :, lo : lo + count],
                    )
                planes_g[s] = g

            def lay_out_x(s, copy):
                xc = work.tile([P, CH, COLS], F32, bufs=4)
                to_planes(xc, loaded[s][3], copy)
                planes_x[s] = xc

            def scale_grad(s, planes):
                if planes[0] == 0:
                    hr = work.tile([P, CH, COLS], F32, bufs=3)
                    state[s]["hr"] = hr
                hr = state[s]["hr"]
                for d in planes:
                    nc.vector.scalar_tensor_tensor(
                        out=hr[:, d, :],
                        in0=planes_g[s][:, d // 2, :, d % 2],
                        scalar=w[:, d : d + 1],
                        in1=rstd_beta[:, 0, :],
                        op0=ALU.mult,
                        op1=ALU.mult,
                    )

            def add_up_hr(s):
                mean_turned = work.tile([P, COLS], F32)
                turn_and_add(state[s]["hr"], CH, hr_r_bank(s)[:, 0, :])
                nc.scalar.activation(out=mean_turned[:], in_=hr_r_bank(s)[:, 0, :], func=COPY, scale=1.0 / CH)
                state[s]["mean_turned"] = mean_turned

            def turn_back_mean(s):
                for b in range(0, COLS, P):
                    nc.tensor.transpose(
                        out=state[s]["mu_mean"][:, 1, b : b + P],
                        in_=state[s]["mean_turned"][:, b : b + P],
                        identity=identity[:],
                    )

            def multiply(s, engine):
                prod = work.tile([P, CH + 1, COLS], F32, bufs=1)
                width = P if s == 0 else COLS
                for b in range(0, COLS, width):
                    engine.tensor_tensor(
                        out=prod[:, :CH, b : b + width],
                        in0=state[s]["hr"][:, :, b : b + width],
                        in1=planes_x[s][:, :, b : b + width],
                        op=ALU.mult,
                    )
                state[s]["prod"] = prod

            def correlate(s):
                prod = state[s]["prod"]
                nc.vector.scalar_tensor_tensor(
                    out=prod[:, CH, :],
                    in0=state[s]["mu_mean"][:, 1, :],
                    scalar=-1.0 * CH,
                    in1=state[s]["m"][:],
                    op0=ALU.mult,
                    op1=ALU.mult,
                )
                turn_and_add(prod, CH + 1, kappa_prod[:, 1, :])

            def slope_b(s):
                kappa_turned = work.tile([P, COLS], F32)
                nc.vector.scalar_tensor_tensor(
                    out=kappa_turned[:],
                    in0=kappa_prod[:, 1, :],
                    scalar=1.0 / CH,
                    in1=state[s]["r_sq_turned"][:],
                    op0=ALU.mult,
                    op1=ALU.mult,
                )
                state[s]["kappa_turned"] = kappa_turned
                for b in range(0, COLS, P):
                    nc.tensor.transpose(
                        out=kappa_prod[:, 0, b : b + P], in_=kappa_turned[:, b : b + P], identity=identity[:]
                    )

            def slope_c(s):
                minus_kappa_mu = work.tile([P, COLS], F32)
                nc.vector.scalar_tensor_tensor(
                    out=minus_kappa_mu[:],
                    in0=state[s]["kappa_turned"][:],
                    scalar=-1.0,
                    in1=state[s]["mu_mean"][:, 0, :],
                    op0=ALU.mult,
                    op1=ALU.mult,
                )
                for b in range(0, COLS, P):
                    for term, first_term in ((state[s]["mean_turned"], True), (minus_kappa_mu, False)):
                        nc.tensor.matmul(
                            out=rstd_beta[:, 1, b : b + P],
                            lhsT=term[:, b : b + P],
                            rhs=identity[:],
                            is_transpose=True,
                            start=first_term,
                            stop=not first_term,
                        )

            def scale_xc(s):
                for lo in range(0, CH, HALF_CH):
                    part = planes_x[s][:, lo : lo + HALF_CH, :]
                    nc.vector.tensor_tensor(
                        out=part, in0=part, in1=over_planes(kappa_prod[:, 0, :], HALF_CH), op=ALU.mult
                    )

            def add_mean(s):
                for lo in range(0, CH, HALF_CH):
                    part = planes_x[s][:, lo : lo + HALF_CH, :]
                    nc.vector.tensor_tensor(
                        out=part, in0=part, in1=over_planes(rstd_beta[:, 1, :], HALF_CH), op=ALU.add
                    )

            def finish_dx(s, engine, planes):
                if planes.start == 0:
                    dx = work.tile([P, CH, COLS], BF16, align_bytes=64, bufs=1)
                    state[s]["dx"] = dx
                engine.tensor_tensor(
                    out=state[s]["dx"][:, planes, :], in0=state[s]["hr"][:, planes, :], in1=planes_x[s][:, planes, :], op=ALU.subtract
                )

            def quantise_dx(s, planes):
                block, part = divmod(s, STEPS_A_BLOCK)
                cols = slice(part * J_STEP, (part + 1) * J_STEP)
                for d in planes:
                    own = window_of(d) + d % HALF_CH
                    nc.vector.quantize_mx(
                        out=dx_codes[block % 2][:, own, cols].bitcast(E5M2_X4),
                        scales=dx_scales[block % 2][:, own, cols],
                        in_=state[s]["dx"][:, d, :],
                    )

            filled = []
            woven_tiles = {}

            def multiply_mx(block, kt, lo, tag):
                if tag == "product":
                    product = sums.tile([P, SIDE], F32, tag=tag, bufs=PRODUCT_BANKS)
                else:
                    product = sums.tile([P, SIDE], F32, tag=tag)
                for q in range(HALF_CH):
                    d = lo + q
                    window = slice(window_of(d), window_of(d) + HALF_CH)
                    nc.tensor.matmul_mx(
                        out=product[:],
                        lhsT=a_codes[:, kt, d, :].bitcast(E4M3_X4),
                        lhsT_scale=a_scales[:, kt, d, :],
                        rhs=dx_codes[block % 2][:, window, :].rearrange("p b j -> p (b j)").bitcast(E5M2_X4),
                        rhs_scale=dx_scales[block % 2][:, window, :].rearrange("p b j -> p (b j)"),
                        start=(q == 0),
                        stop=(q == HALF_CH - 1),
                    )
                filled.append((product, block, kt, lo))

            def mask_and_store():
                product, block, kt, lo = filled[0]
                filled.remove(filled[0])
                if lo == 0:
                    woven = stores.tile([P, J_BLOCK, CH], F32)
                    woven_tiles[(block, kt)] = woven
                woven = woven_tiles[(block, kt)]
                pieces = 2 if (block, kt) == (BLOCKS - 1, K_TILES - 1) and lo > 0 else 1
                width = J_BLOCK // pieces
                for j in range(0, J_BLOCK, width):
                    first_j = block * J_BLOCK + j
                    nc.vector.tensor_tensor(
                        out=woven[:, j : j + width, lo : lo + HALF_CH],
                        in0=product[:].rearrange("p (d j) -> p j d", d=HALF_CH)[:, j : j + width, :],
                        in1=mask_kj_sb[:, kt, first_j : first_j + width].unsqueeze(2).to_broadcast([P, width, HALF_CH]),
                        op=ALU.mult,
                    )
                    if lo > 0:
                        nc.sync.dma_start(
                            out=out_rows[kt][:, first_j * CH : (first_j + width) * CH],
                            in_=woven[:, j : j + width, :].rearrange("p j d -> p (j d)"),
                        )

            a_tiles = {}

            def load_a(kt):
                a_ld = loads.tile([P, PACK, K_TILE, CH], BF16)
                nc.sync.dma_start(out=a_ld[:], in_=a_rows[:, :, kt * K_TILE : (kt + 1) * K_TILE, :])
                a_tiles[kt] = a_ld

            planes_a = {}
            keeps = {}

            def lay_out_a(kt, lo):
                if lo == 0:
                    keep_ik = work.tile([P, K_TILE * PACK], BF16, bufs=1)
                    nc.scalar.copy(
                        out=keep_ik[:].rearrange("p (k t) -> p k t", t=PACK),
                        in_=mask_ik_sb[:, :, kt * K_TILE : (kt + 1) * K_TILE].rearrange("p t k -> p k t"),
                    )
                    keeps[kt] = keep_ik
                    a_planes = work.tile([P, CH, K_TILE * PACK], BF16, align_bytes=64)
                    planes_a[kt] = a_planes
                nc.scalar.copy(
                    out=planes_a[kt][:, lo : lo + HALF_CH, :].rearrange("p d (c t) -> p c t d", t=PACK),
                    in_=a_tiles[kt][:, :, :, lo : lo + HALF_CH].rearrange("p t c d -> p c t d"),
                )

            def stage_keep(kt):
                keep_ps = sums.tile([P, K_TILE * PACK], BF16)
                nc.tensor.matmul(out=keep_ps[:], lhsT=identity_bf16[:], rhs=keeps[kt][:], start=True, stop=True)
                keeps[kt] = keep_ps

            def mask_a(kt):
                a_planes = planes_a[kt]
                nc.vector.tensor_tensor(
                    out=a_planes[:],
                    in0=a_planes[:],
                    in1=keeps[kt][:].unsqueeze(1).to_broadcast([P, CH, K_TILE * PACK]),
                    op=ALU.mult,
                )

            def quantise_a(kt):
                nc.vector.quantize_mx(
                    out=a_codes[:, kt, :, :].rearrange("p d k -> p (d k)").bitcast(E4M3_X4),
                    scales=a_scales[:, kt, :, :].rearrange("p d k -> p (d k)"),
                    in_=planes_a[kt][:].rearrange("p d c -> p (d c)"),
                )

            waiting = [
                (block, kt, lo) for block in range(BLOCKS) for kt in range(K_TILES) for lo in range(0, CH, HALF_CH)
            ]

            def products_of(turn):
                chosen = []
                while waiting and len(chosen) < PRODUCTS_A_TURN:
                    block, kt, lo = waiting[0]
                    dx_turn = (block + 1) * STEPS_A_BLOCK - 1 + 2
                    a_turn = A_FIRST_TURN + kt + 1
                    if max(dx_turn, a_turn) >= turn:
                        break
                    chosen.append(waiting[0])
                    waiting.remove(waiting[0])
                return chosen

            load(0)
            load(1)
            copy_rstd(0)
            stage_rstd(0)
            w_spread = sums.tile([P, CH], F32, tag="mu_mean")
            nc.tensor.matmul(out=w_spread[:], lhsT=ones[:], rhs=w_row[:], start=True, stop=True)
            nc.vector.tensor_copy(out=w[:], in_=w_spread[:])
            lay_out_g(0)
            copy_mu(0)
            def empty(count, leave=1):
                for i in range(min(count, len(filled) - leave)):
                    mask_and_store()

            for turn in range(STEPS):
                first, second, third = turn, turn - 1, turn - 2
                to_fill = products_of(turn)

                def fill(count):
                    for i in range(min(count, len(to_fill))):
                        bank = to_fill[0]
                        to_fill.remove(bank)
                        multiply_mx(*bank, "product")

                if turn == 0:
                    nc.sync.dma_start(out=mask_ik_sb[:], in_=mask_ik_rows)
                    load_a(0)
                if turn + 2 < STEPS:
                    load(turn + 2)
                for kt in a_tiles_laid_out_in(turn + 1):
                    if kt > 0:
                        load_a(kt)
                if turn == 2:
                    nc.sync.dma_start(out=mask_kj_sb[:], in_=mask_kj_rows)
                if 0 <= third:
                    finish_dx(third, nc.gpsimd, slice(0, CH))
                if turn == 1:
                    lay_out_a(0, 0)
                if first + 1 < STEPS:
                    copy_rstd(first + 1)
                    copy_mu(first + 1)
                    if turn > 1:
                        lay_out_g(first + 1)
                fill(1)
                scale_grad(first, (0, 1, 2, 3, 4, 5))
                if 0 <= second:
                    slope_b(second)
                scale_grad(first, (6, 7))
                if 0 <= second:
                    slope_c(second)
                add_up_hr(first)
                if turn <= 1:
                    lay_out_g(first + 1)
                if turn == 0:
                    stage_rstd(1)
                empty(1)
                for kt in a_tiles_laid_out_in(turn - 1):
                    mask_a(kt)
                if turn == 0:
                    lay_out_x(0, nc.vector.tensor_copy)
                stage_pairs(first)
                fill(1)
                turn_back_mean(first)
                turn_rstd(first)
                multiply(first, nc.gpsimd if turn > 0 else nc.vector)
                if turn <= 1:
                    square_rstd(first)
                for kt in a_tiles_laid_out_in(turn):
                    if turn > 1:
                        lay_out_a(kt, 0)
                    lay_out_a(kt, HALF_CH)
                if turn > 1:
                    square_rstd(first)
                if first + 1 < STEPS:
                    lay_out_x(first + 1, nc.scalar.copy)
                if 0 <= second:
                    scale_xc(second)
                fill(2)
                empty(1)
                fill(1)
                if 0 <= second:
                    add_mean(second)
                empty(1)
                if 0 < turn and first + 1 < STEPS:
                    stage_rstd(first + 1)
                fill(PRODUCTS_A_TURN)
                correlate(first)
                for kt in a_tiles_laid_out_in(turn):
                    stage_keep(kt)
                empty(1)
                for kt in a_tiles_laid_out_in(turn - 1):
                    quantise_a(kt)
                if 0 <= third:
                    quantise_dx(third, range(CH))
                empty(PRODUCTS_A_TURN)

            bank_cycle = ["keep_ps", "hr_r"] + PRODUCT_BANKS * ["product"] + ["mu_mean"]

            def fill(count):
                for i in range(min(count, len(waiting))):
                    bank = waiting[0]
                    waiting.remove(bank)
                    multiply_mx(*bank, bank_cycle[0])
                    bank_cycle.append(bank_cycle[0])
                    bank_cycle.remove(bank_cycle[0])

            last = STEPS - 1
            finish_dx(last - 1, nc.gpsimd, slice(0, CH))
            fill(1)
            slope_b(last)
            slope_c(last)
            fill(1)
            empty(1)
            fill(3)
            scale_xc(last)
            empty(1)
            fill(2)
            add_mean(last)
            empty(1)
            fill(1)
            quantise_dx(last - 1, range(CH))
            empty(1)
            waiting = sorted(waiting, key=lambda bank: (bank[1] // 2, bank[2], bank[1]))
            for lo in range(0, CH, HALF_CH):
                finish_dx(last, nc.vector, slice(lo, lo + HALF_CH))
                empty(1)
                quantise_dx(last, range(lo, lo + HALF_CH))
                fill(2)
            fill(len(waiting))
            empty(len(filled), 0)
